import numpy as np
import ml_dtypes


def mxq(x, axis, fmt="e4m3"):
    dtype, down = {"e4m3": (ml_dtypes.float8_e4m3fn, 7), "e5m2": (ml_dtypes.float8_e5m2, 14)}[fmt]
    v = np.moveaxis(np.asarray(x, np.float32).astype(ml_dtypes.bfloat16).astype(np.float64), axis, -1)
    blocks = v.reshape(v.shape[:-1] + (-1, 32))
    amax = np.abs(blocks).max(-1, keepdims=True)
    byte = np.maximum(np.where(amax > 0, np.frexp(amax)[1] - 1 + 127, 0) - down, 1)
    scale = np.exp2(byte - 127.0)
    codes = (blocks / scale).astype(np.float32).astype(dtype).astype(np.float64)
    return np.moveaxis((codes * scale).reshape(v.shape), -1, axis)


WIDE = False


def mx_kscale(k):
    if not WIDE:
        return np.ones(k)
    levels = np.array([18, -18])
    if k % 512:
        return np.exp2(np.random.permutation(np.resize(levels, k // 32))).repeat(32)
    a = np.empty((k // 512, 16))
    for p in range(k // 512):
        a[p, :8] = np.random.permutation(np.resize(levels, 8))
        for g in range(8):
            far = levels[np.abs(levels - a[p, g]) >= 10]
            a[p, g + 8] = far[np.random.randint(len(far))]
    return np.exp2(a.ravel()).repeat(32)


BF16 = ml_dtypes.bfloat16


def bf(x):
    return np.asarray(x, np.float32).astype(BF16)


def f64(x):
    return np.asarray(x).astype(np.float64)


B, EMBED, DETER, STOC, HID = 512, 1536, 1024, 256, 1024
DIST = 2 * STOC
CAT = DETER + EMBED


def softplus(v):
    return np.maximum(v, 0.0) + np.log(1.0 + np.exp(-np.abs(v)))


def sigmoid(v):
    return 1.0 / (1.0 + np.exp(-v))


def setup_inputs():
    s = mx_kscale(B)[:, None]
    u = mx_kscale(DIST)
    v = mx_kscale(HID)
    r = np.random.standard_normal
    h0 = bf(r((B, DETER)) * 0.65)
    e0 = bf(r((B, EMBED)))
    wp1 = bf(r((HID, DETER)) / np.sqrt(DETER))
    bp1 = bf(r(HID) * 0.1)
    wp2 = bf(r((DIST, HID)) / np.sqrt(HID))
    bp2 = bf(r(DIST) * 0.1)
    wq1_0 = bf(r((HID, CAT)) / np.sqrt(CAT))
    bq1 = bf(r(HID) * 0.1)
    wq2_0 = bf(r((DIST, HID)) / np.sqrt(HID))
    bq2 = bf(r(DIST) * 0.1)
    zq = np.concatenate([f64(h0), f64(e0)], -1) @ f64(wq1_0).T + f64(bq1)
    vq = (np.maximum(zq, 0.0) @ f64(wq2_0).T + f64(bq2))[:, STOC:]

    def grad():
        return r((B, STOC)) * np.exp2(np.random.randint(-6, 1, (B, 1))) * 4.0

    g0 = bf(grad() / s * u[:STOC])
    g1 = bf(grad() / s * u[STOC:])
    g2 = bf(grad())
    g3 = bf(grad())
    return {
        "h": bf(f64(h0) * s),
        "embedding": bf(f64(e0) * s),
        "wp1": wp1,
        "bp1": bp1,
        "wp2": wp2,
        "bp2": bp2,
        "wq1": bf(f64(wq1_0) / v[:, None]),
        "bq1": bq1,
        "wq2": bf(f64(wq2_0) / u[:, None] * v),
        "bq2": bq2,
        "zq": np.asarray(zq, np.float32),
        "vq": np.asarray(vq, np.float32),
        "grad_0": g0,
        "grad_1": g1,
        "grad_2": g2,
        "grad_3": g3,
    }


def reference(h, embedding, wp1, bp1, wp2, bp2, wq1, bq1, wq2, bq2, zq, vq, grad_0, grad_1, grad_2, grad_3):
    dz2 = np.concatenate([f64(grad_0), f64(grad_1) * sigmoid(f64(vq))], -1)
    da = mxq(dz2, 1, "e5m2") @ mxq(f64(wq2), 0, "e4m3")
    dz1 = np.where(f64(zq) > 0.0, da, 0.0)
    de = mxq(dz1, 1, "e5m2") @ mxq(f64(wq1)[:, DETER:], 0, "e4m3")
    c = np.concatenate([f64(h), f64(embedding)], -1)
    dwq1 = mxq(dz1, 0, "e5m2").T @ mxq(c, 0, "e4m3")
    return de, dwq1

@@ -1,0 +1,217 @@
+from contextlib import ExitStack
+
+import concourse.mybir as mybir
+from concourse.masks import make_identity
+
+B, EMBED, DETER, STOC, HID = 512, 1536, 1024, 256, 1024
+DIST = 2 * STOC
+
+FLOPS = 2 * (B * DIST * HID + B * HID * EMBED + HID * B * (DETER + EMBED))
+BYTES = 2 * (2 * B * STOC + DIST * HID + HID * EMBED + B * (DETER + EMBED)) + 4 * (B * STOC + B * HID) + 4 * (B * EMBED + HID * (DETER + EMBED))
+
+F32 = mybir.dt.float32
+BF16 = mybir.dt.bfloat16
+U32 = mybir.dt.uint32
+U8 = mybir.dt.uint8
+E4M3 = mybir.dt.float8_e4m3fn_x4
+E5M2 = mybir.dt.float8_e5m2_x4
+MULT = mybir.AluOpType.mult
+IS_GT = mybir.AluOpType.is_gt
+SIGMOID = mybir.ActivationFunctionType.Sigmoid
+
+P = 128
+PACK = 4
+COLS = 512
+VFROM = 6
+STAGED = {2: 5, 3: 4}
+
+
+def tile_rssmcell_pb_v_kernel(tc, h, embedding, wp1, bp1, wp2, bp2, wq1, bq1, wq2, bq2, zq, vq, grad_0, grad_1, grad_2, grad_3, out_0, out_1):
+    nc = tc.nc
+    with ExitStack() as ctx:
+        keep = ctx.enter_context(tc.tile_pool(name="keep", bufs=1))
+        grouping = ctx.enter_context(tc.tile_pool(name="grouping", bufs=6))
+        staging = ctx.enter_context(tc.tile_pool(name="staging", bufs=4))
+        psum = ctx.enter_context(tc.psum_pool(name="psum", bufs=8))
+        ctx.enter_context(tc.manual_schedule())
+
+        def rows4(ap):
+            return ap.rearrange("(p j) w -> p j w", j=PACK)
+
+        def operand(name):
+            codes = keep.tile([P, COLS], U32, name=name + "_codes", align_bytes=64)
+            scales = keep.tile([P, COLS], U8, name=name + "_scales", align_bytes=64)
+            return codes, scales
+
+        def new_grouped():
+            grouped = grouping.tile([P, COLS, PACK], BF16, name="grouped", align_bytes=64)
+            return grouped
+
+        def interleave(copy, rows):
+            grouped = new_grouped()
+            copy(out=grouped[:].rearrange("p (c i) t -> p c t i", i=4), in_=rows.rearrange("p t (c i) -> p c t i", i=4))
+            return grouped
+
+        def quantize(target, grouped, fmt):
+            codes, scales = target
+            nc.vector.quantize_mx(out=codes[:].bitcast(fmt), scales=scales[:], in_=grouped[:].rearrange("p w t -> p (w t)"))
+
+        def transpose_pair(rows, pair):
+            bank = psum.tile([P, COLS], F32, name="bank")
+            for jj in range(2):
+                words = rows[:, 2 * pair + jj, :].bitcast(F32)
+                for u in range(2):
+                    at = P * (2 * jj + u)
+                    nc.tensor.transpose(bank[:, at : at + P], words[:, u::2], ident[:])
+            return bank
+
+        def gather_pair(copy, grouped, pair, bank):
+            words = grouped[:].rearrange("p w t -> p (w t)").bitcast(F32)
+            copy(out=words[:, COLS * pair : COLS * (pair + 1)].rearrange("p (j r u) -> p j r u", j=2, u=2), in_=bank[:].rearrange("p (j u r) -> p j r u", j=2, u=2))
+
+        def mx(bank, stationary, m, moving, start, stop):
+            cols = slice(P * m, P * (m + 1))
+            nc.tensor.matmul_mx(
+                out=bank[:],
+                lhsT=stationary[0][:, cols].bitcast(E5M2),
+                lhsT_scale=stationary[1][:, cols],
+                rhs=moving[0][:].bitcast(E4M3),
+                rhs_scale=moving[1][:],
+                start=start,
+                stop=stop,
+            )
+
+        vcopy, scopy = nc.vector.tensor_copy, nc.scalar.copy
+
+        v_raw = keep.tile([P, PACK, STOC], F32, name="v_raw")
+        nc.sync.dma_start(out=v_raw[:], in_=rows4(vq))
+        g0_raw = keep.tile([P, PACK, STOC], BF16, name="g0_raw")
+        nc.sync.dma_start(out=g0_raw[:], in_=rows4(grad_0))
+        g1_raw = keep.tile([P, PACK, STOC], BF16, name="g1_raw")
+        nc.sync.dma_start(out=g1_raw[:], in_=rows4(grad_1))
+        dz2 = keep.tile([P, PACK, DIST], BF16, name="dz2")
+        wq2_raw = keep.tile([P, PACK, HID], BF16, name="wq2_raw")
+        nc.sync.dma_start(out=wq2_raw[:], in_=rows4(wq2))
+        h_raw = keep.tile([P, PACK, DETER], BF16, name="h_raw")
+        nc.sync.dma_start(out=h_raw[:], in_=rows4(h))
+        z_raw = []
+        for pair in range(2):
+            z = keep.tile([P, 2, HID], F32, name="z_raw%d" % pair)
+            nc.sync.dma_start(out=z[:], in_=rows4(zq)[:, 2 * pair : 2 * pair + 2, :])
+            z_raw.append(z)
+        e_raw = keep.tile([P, PACK, EMBED], BF16, name="e_raw")
+        nc.sync.dma_start(out=e_raw[:], in_=rows4(embedding))
+        w_raw = []
+        for g in range(2):
+            w = keep.tile([P, PACK, EMBED], BF16, name="w_raw%d" % g)
+            nc.sync.dma_start(out=w[:], in_=rows4(wq1[COLS * g : COLS * (g + 1), DETER:]))
+            w_raw.append(w)
+
+        ident = keep.tile([P, P], F32, name="ident")
+        make_identity(nc, ident[:])
+
+        sig = keep.tile([P, PACK, STOC], F32, name="sig")
+        vcopy(out=dz2[:, :, 0:STOC], in_=g0_raw[:])
+        for pair in range(2):
+            js = slice(2 * pair, 2 * pair + 2)
+            nc.scalar.activation(out=sig[:, js, :], in_=v_raw[:, js, :], func=SIGMOID)
+            nc.vector.tensor_tensor(out=dz2[:, js, STOC:], in0=g1_raw[:, js, :], in1=sig[:, js, :], op=MULT)
+        banks = [transpose_pair(dz2, pair) for pair in range(2)]
+        w2_grouped = [interleave(vcopy, wq2_raw[:, :, 0:COLS])]
+        dz2_grouped = new_grouped()
+        for pair in range(2):
+            gather_pair(scopy, dz2_grouped, pair, banks[pair])
+        w2_op = [operand("w2_0"), operand("w2_1")]
+        quantize(w2_op[0], w2_grouped[0], E4M3)
+        dz2_op = operand("dz2")
+        quantize(dz2_op, dz2_grouped, E5M2)
+        w2_grouped.append(interleave(scopy, wq2_raw[:, :, COLS:]))
+
+        dz1_tok = [operand("dz1_tok%d" % g) for g in range(2)]
+        dz1_hid = [operand("dz1_hid%d" % g) for g in range(2)]
+        c_op = [operand("c%d" % n) for n in range(5)]
+        w1_op = [[operand("w1_%d_%d" % (g, n)) for n in range(3)] for g in range(2)]
+        dz1 = [keep.tile([P, PACK, COLS], BF16, name="dz1_%d" % g) for g in range(2)]
+
+        def da_banks(g, pair):
+            banks = []
+            for j in (2 * pair, 2 * pair + 1):
+                bank = psum.tile([P, COLS], F32, name="bank")
+                mx(bank, dz2_op, j, w2_op[g], True, True)
+                banks.append(bank)
+            return banks
+
+        def mask(g, pair, banks):
+            for jj in range(2):
+                nc.vector.scalar_tensor_tensor(out=dz1[g][:, 2 * pair + jj, :], in0=z_raw[pair][:, jj, COLS * g : COLS * (g + 1)], scalar=0.0, in1=banks[jj][:], op0=IS_GT, op1=MULT)
+
+        da = [[da_banks(0, 0)], []]
+        quantize(w2_op[1], w2_grouped[1], E4M3)
+        da[1].append(da_banks(1, 0))
+        da[0].append(da_banks(0, 1))
+        da[1].append(da_banks(1, 1))
+        h_grouped = [interleave(scopy, h_raw[:, :, 0:COLS]), interleave(scopy, h_raw[:, :, COLS:])]
+        mask(0, 0, da[0][0])
+        mask(1, 0, da[1][0])
+        hid_grouped = [new_grouped(), new_grouped()]
+        for g in range(2):
+            bank = transpose_pair(dz1[g], 0)
+            gather_pair(scopy, hid_grouped[g], 0, bank)
+        mask(0, 1, da[0][1])
+        tok_grouped = [interleave(vcopy, dz1[0][:])]
+        quantize(c_op[0], h_grouped[0], E4M3)
+        quantize(dz1_tok[0], tok_grouped[0], E5M2)
+        bank = transpose_pair(dz1[0], 1)
+        gather_pair(scopy, hid_grouped[0], 1, bank)
+        quantize(c_op[1], h_grouped[1], E4M3)
+        mask(1, 1, da[1][1])
+        tok_grouped.append(interleave(vcopy, dz1[1][:]))
+
+        def evacuate(copy, out, bank):
+            copy(out=out, in_=bank[:])
+
+        def out1_tile(m, first, count, copies):
+            staged = staging.tile([P, count * COLS], F32, name="staged%d" % count, bufs=STAGED[count])
+            for n in range(count):
+                bank = psum.tile([P, COLS], F32, name="bank")
+                mx(bank, dz1_tok[m // 4], m % 4, c_op[first + n], True, True)
+                evacuate(copies[n], staged[:, COLS * n : COLS * (n + 1)], bank)
+            nc.sync.dma_start(out=out_1[P * m : P * (m + 1), COLS * first : COLS * (first + count)], in_=staged[:])
+
+        split = 8
+        e_grouped = []
+        for m in range(split):
+            if m == 2:
+                e_grouped.append(interleave(vcopy, e_raw[:, :, 0:COLS]))
+                quantize(dz1_tok[1], tok_grouped[1], E5M2)
+            out1_tile(m, 0, 2, (scopy,) * 2)
+            if m == 1:
+                bank = transpose_pair(dz1[1], 1)
+                gather_pair(scopy, hid_grouped[1], 1, bank)
+        e_grouped.append(interleave(vcopy, e_raw[:, :, COLS : 2 * COLS]))
+        quantize(c_op[2], e_grouped[0], E4M3)
+        e_grouped.append(interleave(vcopy, e_raw[:, :, 2 * COLS :]))
+        quantize(c_op[3], e_grouped[1], E4M3)
+        quantize(dz1_hid[0], hid_grouped[0], E5M2)
+        quantize(c_op[4], e_grouped[2], E4M3)
+        quantize(dz1_hid[1], hid_grouped[1], E5M2)
+        chunks = [(g, n) for n in range(3) for g in range(2)]
+        w_grouped = []
+        for m in range(8):
+            if m < 6:
+                g, n = chunks[m]
+                w_grouped.append(interleave(vcopy, w_raw[g][:, :, COLS * n : COLS * (n + 1)]))
+            out1_tile(m, 2, 3, (scopy, vcopy, scopy) if m > 6 else (scopy,) * 3)
+            if m >= 1 and m < 7:
+                g, n = chunks[m - 1]
+                quantize(w1_op[g][n], w_grouped[m - 1], E4M3)
+
+        for pair in range(2):
+            staged = staging.tile([P, 2, EMBED], F32, name="staged_out0", bufs=2)
+            for jj in range(2):
+                for n in range(3):
+                    bank = psum.tile([P, COLS], F32, name="bank")
+                    for g in range(2):
+                        mx(bank, dz1_hid[g], 2 * pair + jj, w1_op[g][n], g == 0, g == 1)
+                    evacuate((scopy, vcopy)[n % 2], staged[:, jj, COLS * n : COLS * (n + 1)], bank)
+            nc.sync.dma_start(out=rows4(out_0)[:, 2 * pair : 2 * pair + 2, :], in_=staged[:])

@@ -22,8 +22,7 @@ SIGMOID = mybir.ActivationFunctionType.Sigmoid
 P = 128
 PACK = 4
 COLS = 512
-VFROM = 6
-STAGED = {2: 5, 3: 4}
+HALF = COLS // 2
 
 
 def tile_rssmcell_pb_v_kernel(tc, h, embedding, wp1, bp1, wp2, bp2, wq1, bq1, wq2, bq2, zq, vq, grad_0, grad_1, grad_2, grad_3, out_0, out_1):
@@ -31,12 +30,18 @@ def tile_rssmcell_pb_v_kernel(tc, h, embedding, wp1, bp1, wp2, bp2, wq1, bq1, wq
     with ExitStack() as ctx:
         keep = ctx.enter_context(tc.tile_pool(name="keep", bufs=1))
         grouping = ctx.enter_context(tc.tile_pool(name="grouping", bufs=6))
-        staging = ctx.enter_context(tc.tile_pool(name="staging", bufs=4))
-        psum = ctx.enter_context(tc.psum_pool(name="psum", bufs=8))
+        staging = ctx.enter_context(tc.tile_pool(name="staging", bufs=6))
+        psum = ctx.enter_context(tc.psum_pool(name="psum", bufs=1))
         ctx.enter_context(tc.manual_schedule())
+        vcopy, scopy = nc.vector.tensor_copy, nc.scalar.copy
 
         def rows4(ap):
             return ap.rearrange("(p j) w -> p j w", j=PACK)
+
+        def load(name, view, dtype):
+            raw = keep.tile([P] + list(view.shape[1:]), dtype, name=name)
+            nc.sync.dma_start(out=raw[:], in_=view)
+            return raw
 
         def operand(name):
             codes = keep.tile([P, COLS], U32, name=name + "_codes", align_bytes=64)
@@ -47,32 +52,52 @@ def tile_rssmcell_pb_v_kernel(tc, h, embedding, wp1, bp1, wp2, bp2, wq1, bq1, wq
             grouped = grouping.tile([P, COLS, PACK], BF16, name="grouped", align_bytes=64)
             return grouped
 
+        def new_bank(free):
+            index = free.pop(0)
+            bank = psum.tile([P, COLS], F32, name="bank%d" % index)
+            return bank, index, free
+
+        def release(held):
+            held[2].append(held[1])
+
+        def new_staged(rows, count):
+            staged = staging.tile([P, rows, count * COLS], F32, name="staged")
+            return staged
+
+        def chunk(raw, n):
+            return raw[:, :, COLS * n : COLS * (n + 1)]
+
+        def interleave_into(copy, grouped, rows):
+            copy(out=grouped.rearrange("p (c i) t -> p c t i", i=4), in_=rows.rearrange("p t (c i) -> p c t i", i=4))
+
         def interleave(copy, rows):
             grouped = new_grouped()
-            copy(out=grouped[:].rearrange("p (c i) t -> p c t i", i=4), in_=rows.rearrange("p t (c i) -> p c t i", i=4))
+            interleave_into(copy, grouped[:], rows)
             return grouped
 
-        def quantize(target, grouped, fmt):
+        def quantize(target, grouped, fmt, cols=slice(0, COLS)):
             codes, scales = target
-            nc.vector.quantize_mx(out=codes[:].bitcast(fmt), scales=scales[:], in_=grouped[:].rearrange("p w t -> p (w t)"))
+            nc.vector.quantize_mx(out=codes[:, cols].bitcast(fmt), scales=scales[:, cols], in_=grouped[:, cols, :].rearrange("p w t -> p (w t)"))
 
-        def transpose_pair(rows, pair):
-            bank = psum.tile([P, COLS], F32, name="bank")
+        def transpose_pair(rows, pair, free):
+            held = new_bank(free)
+            bank = held[0]
             for jj in range(2):
                 words = rows[:, 2 * pair + jj, :].bitcast(F32)
                 for u in range(2):
                     at = P * (2 * jj + u)
                     nc.tensor.transpose(bank[:, at : at + P], words[:, u::2], ident[:])
-            return bank
+            return held
 
-        def gather_pair(copy, grouped, pair, bank):
+        def gather_pair(copy, grouped, pair, held):
             words = grouped[:].rearrange("p w t -> p (w t)").bitcast(F32)
-            copy(out=words[:, COLS * pair : COLS * (pair + 1)].rearrange("p (j r u) -> p j r u", j=2, u=2), in_=bank[:].rearrange("p (j u r) -> p j r u", j=2, u=2))
+            copy(out=words[:, COLS * pair : COLS * (pair + 1)].rearrange("p (j r u) -> p j r u", j=2, u=2), in_=held[0][:].rearrange("p (j u r) -> p j r u", j=2, u=2))
+            release(held)
 
-        def mx(bank, stationary, m, moving, start, stop):
+        def mx(held, stationary, m, moving, start, stop):
             cols = slice(P * m, P * (m + 1))
             nc.tensor.matmul_mx(
-                out=bank[:],
+                out=held[0][:],
                 lhsT=stationary[0][:, cols].bitcast(E5M2),
                 lhsT_scale=stationary[1][:, cols],
                 rhs=moving[0][:].bitcast(E4M3),
@@ -81,137 +106,167 @@ def tile_rssmcell_pb_v_kernel(tc, h, embedding, wp1, bp1, wp2, bp2, wq1, bq1, wq
                 stop=stop,
             )
 
-        vcopy, scopy = nc.vector.tensor_copy, nc.scalar.copy
+        def da_banks(g):
+            banks = []
+            for j in range(PACK):
+                bank = new_bank(v_free)
+                mx(bank, dz2_op, j, w2_op[g], True, True)
+                banks.append(bank)
+            return banks
 
-        v_raw = keep.tile([P, PACK, STOC], F32, name="v_raw")
-        nc.sync.dma_start(out=v_raw[:], in_=rows4(vq))
-        g0_raw = keep.tile([P, PACK, STOC], BF16, name="g0_raw")
-        nc.sync.dma_start(out=g0_raw[:], in_=rows4(grad_0))
-        g1_raw = keep.tile([P, PACK, STOC], BF16, name="g1_raw")
-        nc.sync.dma_start(out=g1_raw[:], in_=rows4(grad_1))
-        dz2 = keep.tile([P, PACK, DIST], BF16, name="dz2")
-        wq2_raw = keep.tile([P, PACK, HID], BF16, name="wq2_raw")
-        nc.sync.dma_start(out=wq2_raw[:], in_=rows4(wq2))
-        h_raw = keep.tile([P, PACK, DETER], BF16, name="h_raw")
-        nc.sync.dma_start(out=h_raw[:], in_=rows4(h))
-        z_raw = []
-        for pair in range(2):
-            z = keep.tile([P, 2, HID], F32, name="z_raw%d" % pair)
-            nc.sync.dma_start(out=z[:], in_=rows4(zq)[:, 2 * pair : 2 * pair + 2, :])
-            z_raw.append(z)
-        e_raw = keep.tile([P, PACK, EMBED], BF16, name="e_raw")
-        nc.sync.dma_start(out=e_raw[:], in_=rows4(embedding))
-        w_raw = []
-        for g in range(2):
-            w = keep.tile([P, PACK, EMBED], BF16, name="w_raw%d" % g)
-            nc.sync.dma_start(out=w[:], in_=rows4(wq1[COLS * g : COLS * (g + 1), DETER:]))
-            w_raw.append(w)
+        def mask(g, j, banks, cols=slice(0, COLS)):
+            nc.vector.scalar_tensor_tensor(out=dz1[g][:, j, cols], in0=z_raw[g][:, j, cols], scalar=0.0, in1=banks[j][0][:, cols], op0=IS_GT, op1=MULT)
+            if cols.stop == COLS:
+                release(banks[j])
+
+        def empty(copy, staged, places, banks):
+            for (r, at), bank in reversed(list(zip(places, banks))):
+                copy(out=staged[:, r, COLS * at : COLS * (at + 1)], in_=bank[0][:])
+                release(bank)
+
+        def out1_banks(pairs, free):
+            banks = []
+            for m, n in pairs:
+                bank = new_bank(free)
+                mx(bank, dz1_tok[m // 4], m % 4, c_op[n], True, True)
+                banks.append(bank)
+            return banks
+
+        def out0_banks(pairs, free):
+            banks = []
+            for j, n in pairs:
+                bank = new_bank(free)
+                for g in range(2):
+                    mx(bank, dz1_hid[g], j, w1_op[g][n], g == 0, g == 1)
+                banks.append(bank)
+            return banks
+
+        def store1(staged, m, rows, first, count):
+            view = out_1[P * m : P * (m + rows), COLS * first : COLS * (first + count)]
+            nc.sync.dma_start(out=view.rearrange("(r p) w -> p r w", p=P), in_=staged[:])
+
+        v_raw = load("v_raw", rows4(vq), F32)
+        g1_raw = load("g1_raw", rows4(grad_1), BF16)
+        g0_raw = load("g0_raw", rows4(grad_0), BF16)
+        w2_raw = [load("w2_raw0", rows4(wq2[:, 0:COLS]), BF16)]
+        h_raw = load("h_raw", rows4(h), BF16)
+        z_raw = [load("z_raw0", rows4(zq[:, 0:COLS]), F32)]
+        w2_raw.append(load("w2_raw1", rows4(wq2[:, COLS:]), BF16))
+        e_raw = load("e_raw", rows4(embedding), BF16)
+        z_raw.append(load("z_raw1", rows4(zq[:, COLS:]), F32))
+        w_raw = [load("w_raw%d" % g, rows4(wq1[COLS * g : COLS * (g + 1), DETER:]), BF16) for g in range(2)]
 
         ident = keep.tile([P, P], F32, name="ident")
         make_identity(nc, ident[:])
 
-        sig = keep.tile([P, PACK, STOC], F32, name="sig")
-        vcopy(out=dz2[:, :, 0:STOC], in_=g0_raw[:])
-        for pair in range(2):
-            js = slice(2 * pair, 2 * pair + 2)
-            nc.scalar.activation(out=sig[:, js, :], in_=v_raw[:, js, :], func=SIGMOID)
-            nc.vector.tensor_tensor(out=dz2[:, js, STOC:], in0=g1_raw[:, js, :], in1=sig[:, js, :], op=MULT)
-        banks = [transpose_pair(dz2, pair) for pair in range(2)]
-        w2_grouped = [interleave(vcopy, wq2_raw[:, :, 0:COLS])]
-        dz2_grouped = new_grouped()
-        for pair in range(2):
-            gather_pair(scopy, dz2_grouped, pair, banks[pair])
         w2_op = [operand("w2_0"), operand("w2_1")]
-        quantize(w2_op[0], w2_grouped[0], E4M3)
         dz2_op = operand("dz2")
-        quantize(dz2_op, dz2_grouped, E5M2)
-        w2_grouped.append(interleave(scopy, wq2_raw[:, :, COLS:]))
-
         dz1_tok = [operand("dz1_tok%d" % g) for g in range(2)]
         dz1_hid = [operand("dz1_hid%d" % g) for g in range(2)]
         c_op = [operand("c%d" % n) for n in range(5)]
         w1_op = [[operand("w1_%d_%d" % (g, n)) for n in range(3)] for g in range(2)]
         dz1 = [keep.tile([P, PACK, COLS], BF16, name="dz1_%d" % g) for g in range(2)]
-
-        def da_banks(g, pair):
-            banks = []
-            for j in (2 * pair, 2 * pair + 1):
-                bank = psum.tile([P, COLS], F32, name="bank")
-                mx(bank, dz2_op, j, w2_op[g], True, True)
-                banks.append(bank)
-            return banks
-
-        def mask(g, pair, banks):
-            for jj in range(2):
-                nc.vector.scalar_tensor_tensor(out=dz1[g][:, 2 * pair + jj, :], in0=z_raw[pair][:, jj, COLS * g : COLS * (g + 1)], scalar=0.0, in1=banks[jj][:], op0=IS_GT, op1=MULT)
-
-        da = [[da_banks(0, 0)], []]
-        quantize(w2_op[1], w2_grouped[1], E4M3)
-        da[1].append(da_banks(1, 0))
-        da[0].append(da_banks(0, 1))
-        da[1].append(da_banks(1, 1))
-        h_grouped = [interleave(scopy, h_raw[:, :, 0:COLS]), interleave(scopy, h_raw[:, :, COLS:])]
-        mask(0, 0, da[0][0])
-        mask(1, 0, da[1][0])
-        hid_grouped = [new_grouped(), new_grouped()]
-        for g in range(2):
-            bank = transpose_pair(dz1[g], 0)
-            gather_pair(scopy, hid_grouped[g], 0, bank)
-        mask(0, 1, da[0][1])
-        tok_grouped = [interleave(vcopy, dz1[0][:])]
-        quantize(c_op[0], h_grouped[0], E4M3)
-        quantize(dz1_tok[0], tok_grouped[0], E5M2)
-        bank = transpose_pair(dz1[0], 1)
-        gather_pair(scopy, hid_grouped[0], 1, bank)
-        quantize(c_op[1], h_grouped[1], E4M3)
-        mask(1, 1, da[1][1])
-        tok_grouped.append(interleave(vcopy, dz1[1][:]))
-
-        def evacuate(copy, out, bank):
-            copy(out=out, in_=bank[:])
-
-        def out1_tile(m, first, count, copies):
-            staged = staging.tile([P, count * COLS], F32, name="staged%d" % count, bufs=STAGED[count])
-            for n in range(count):
-                bank = psum.tile([P, COLS], F32, name="bank")
-                mx(bank, dz1_tok[m // 4], m % 4, c_op[first + n], True, True)
-                evacuate(copies[n], staged[:, COLS * n : COLS * (n + 1)], bank)
-            nc.sync.dma_start(out=out_1[P * m : P * (m + 1), COLS * first : COLS * (first + count)], in_=staged[:])
-
-        split = 8
-        e_grouped = []
-        for m in range(split):
-            if m == 2:
-                e_grouped.append(interleave(vcopy, e_raw[:, :, 0:COLS]))
-                quantize(dz1_tok[1], tok_grouped[1], E5M2)
-            out1_tile(m, 0, 2, (scopy,) * 2)
-            if m == 1:
-                bank = transpose_pair(dz1[1], 1)
-                gather_pair(scopy, hid_grouped[1], 1, bank)
-        e_grouped.append(interleave(vcopy, e_raw[:, :, COLS : 2 * COLS]))
-        quantize(c_op[2], e_grouped[0], E4M3)
-        e_grouped.append(interleave(vcopy, e_raw[:, :, 2 * COLS :]))
-        quantize(c_op[3], e_grouped[1], E4M3)
-        quantize(dz1_hid[0], hid_grouped[0], E5M2)
-        quantize(c_op[4], e_grouped[2], E4M3)
-        quantize(dz1_hid[1], hid_grouped[1], E5M2)
-        chunks = [(g, n) for n in range(3) for g in range(2)]
-        w_grouped = []
-        for m in range(8):
-            if m < 6:
-                g, n = chunks[m]
-                w_grouped.append(interleave(vcopy, w_raw[g][:, :, COLS * n : COLS * (n + 1)]))
-            out1_tile(m, 2, 3, (scopy, vcopy, scopy) if m > 6 else (scopy,) * 3)
-            if m >= 1 and m < 7:
-                g, n = chunks[m - 1]
-                quantize(w1_op[g][n], w_grouped[m - 1], E4M3)
+        dz2 = keep.tile([P, PACK, DIST], BF16, name="dz2")
+        sig = keep.tile([P, PACK, STOC], F32, name="sig")
+        s_free, v_free = [0, 1, 2, 3], [4, 5, 6, 7]
+        halves = (slice(0, HALF), slice(HALF, COLS))
 
         for pair in range(2):
-            staged = staging.tile([P, 2, EMBED], F32, name="staged_out0", bufs=2)
-            for jj in range(2):
-                for n in range(3):
-                    bank = psum.tile([P, COLS], F32, name="bank")
-                    for g in range(2):
-                        mx(bank, dz1_hid[g], 2 * pair + jj, w1_op[g][n], g == 0, g == 1)
-                    evacuate((scopy, vcopy)[n % 2], staged[:, jj, COLS * n : COLS * (n + 1)], bank)
+            js = slice(2 * pair, 2 * pair + 2)
+            nc.scalar.activation(out=sig[:, js, :], in_=v_raw[:, js, :], func=SIGMOID)
+            nc.vector.tensor_tensor(out=dz2[:, js, STOC:], in0=g1_raw[:, js, :], in1=sig[:, js, :], op=MULT)
+        scopy(out=dz2[:, :, 0:STOC], in_=g0_raw[:])
+        banks = [transpose_pair(dz2, pair, s_free) for pair in range(2)]
+        w2_grouped = [new_grouped()]
+        for copy, cols in zip((vcopy, scopy), halves):
+            interleave_into(copy, w2_grouped[0][:, cols, :], w2_raw[0][:, :, cols])
+        dz2_grouped = new_grouped()
+        for pair in range(2):
+            gather_pair(scopy, dz2_grouped, pair, banks[pair])
+        quantize(w2_op[0], w2_grouped[0], E4M3)
+        for pair in range(2):
+            quantize(dz2_op, dz2_grouped, E5M2, halves[pair])
+        h_grouped = [interleave(scopy, chunk(h_raw, n)) for n in range(2)]
+        w2_grouped.append(interleave(scopy, w2_raw[1][:]))
+
+        def w1_rows(n, g):
+            return interleave(vcopy, chunk(w_raw[g], n))
+
+        def hid_gather(copy, g, pair, free):
+            gather_pair(copy, hid_grouped[g], pair, transpose_pair(dz1[g], pair, free))
+
+        def out1_pair(staged, m, first, n):
+            empty(scopy, staged, [(r, n - first) for r in range(2)], out1_banks([(m + r, n) for r in range(2)], s_free))
+
+        def out1_rows(m):
+            staged = new_staged(1, 5)
+            empty(scopy, staged, [(0, n) for n in range(0, 2)], out1_banks([(m, n) for n in range(0, 2)], s_free))
+            empty(scopy, staged, [(0, n) for n in range(2, 5)], out1_banks([(m, n) for n in range(2, 5)], s_free))
+            store1(staged, m, 1, 0, 5)
+
+        da = da_banks(0)
+        for j in range(PACK):
+            mask(0, j, da, halves[0])
+        quantize(c_op[0], h_grouped[0], E4M3)
+        tok_grouped = new_grouped()
+        interleave_into(vcopy, tok_grouped[:, halves[0], :], dz1[0][:, :, halves[0]])
+        mask(0, 0, da, halves[1])
+        quantize(dz1_tok[0], tok_grouped, E5M2, halves[0])
+        for j in range(1, PACK):
+            mask(0, j, da, halves[1])
+        quantize(c_op[1], h_grouped[1], E4M3)
+        interleave_into(vcopy, tok_grouped[:, halves[1], :], dz1[0][:, :, halves[1]])
+        e_grouped = [interleave(vcopy, chunk(e_raw, 0))]
+        quantize(dz1_tok[0], tok_grouped, E5M2, halves[1])
+        quantize(w2_op[1], w2_grouped[1], E4M3)
+        quantize(c_op[2], e_grouped[0], E4M3)
+        hid_grouped = [new_grouped()]
+        staged = new_staged(2, 2)
+        for n in range(2):
+            out1_pair(staged, 0, 0, n)
+        store1(staged, 0, 2, 0, 2)
+        for pair in range(2):
+            hid_gather(scopy, 0, pair, s_free)
+        staged = new_staged(2, 2)
+        for n in range(2):
+            out1_pair(staged, 2, 0, n)
+        store1(staged, 2, 2, 0, 2)
+        da = da_banks(1)
+        e_grouped.append(interleave(vcopy, chunk(e_raw, 1)))
+        e_grouped.append(interleave(vcopy, chunk(e_raw, 2)))
+        quantize(c_op[3], e_grouped[1], E4M3)
+        quantize(c_op[4], e_grouped[2], E4M3)
+        for j in reversed(range(PACK)):
+            mask(1, j, da)
+        quantize(dz1_hid[0], hid_grouped[0], E5M2)
+        tok_grouped = interleave(vcopy, dz1[1][:])
+        hid_grouped.append(new_grouped())
+        for m in (0, 2):
+            staged = new_staged(2, 3)
+            if m == 2:
+                s_free.extend([v_free.pop(0), v_free.pop(0)])
+            for n in range(2, 5):
+                out1_pair(staged, m, 2, n)
+                if m == 2 and n == 3:
+                    hid_gather(vcopy, 1, 0, v_free)
+                    quantize(dz1_tok[1], tok_grouped, E5M2)
+                    hid_gather(vcopy, 1, 1, v_free)
+            store1(staged, m, 2, 2, 3)
+
+        for n in range(3):
+            w_grouped = [w1_rows(n, g) for g in range(2)]
+            if n == 0:
+                quantize(dz1_hid[1], hid_grouped[1], E5M2)
+            for g in range(2):
+                quantize(w1_op[g][n], w_grouped[g], E4M3)
+        for m in range(4, 8):
+            out1_rows(m)
+
+        for pair in range(2):
+            staged = new_staged(2, 3)
+            for n in range(3):
+                on_vector = n + pair >= 2
+                empty(vcopy if on_vector else scopy, staged, [(r, n) for r in range(2)], out0_banks([(2 * pair + r, n) for r in range(2)], v_free if on_vector else s_free))
+                if pair == 0 and n == 1:
+                    v_free.extend([s_free.pop(0), s_free.pop(0)])
             nc.sync.dma_start(out=rows4(out_0)[:, 2 * pair : 2 * pair + 2, :], in_=staged[:])

@@ -106,18 +106,18 @@ def tile_rssmcell_pb_v_kernel(tc, h, embedding, wp1, bp1, wp2, bp2, wq1, bq1, wq
                 stop=stop,
             )
 
-        def da_banks(g):
+        def da_banks(g, free):
             banks = []
             for j in range(PACK):
-                bank = new_bank(v_free)
+                bank = new_bank(free)
                 mx(bank, dz2_op, j, w2_op[g], True, True)
                 banks.append(bank)
             return banks
 
         def mask(g, j, banks, cols=slice(0, COLS)):
-            nc.vector.scalar_tensor_tensor(out=dz1[g][:, j, cols], in0=z_raw[g][:, j, cols], scalar=0.0, in1=banks[j][0][:, cols], op0=IS_GT, op1=MULT)
+            nc.vector.scalar_tensor_tensor(out=dz1[g][:, j, cols], in0=z_raw[j // 2][:, j % 2, COLS * g + cols.start : COLS * g + cols.stop], scalar=0.0, in1=banks[j][0][:, cols], op0=IS_GT, op1=MULT)
             if cols.stop == COLS:
-                release(banks[j])
+                s_free.append(banks[j][1])
 
         def empty(copy, staged, places, banks):
             for (r, at), bank in reversed(list(zip(places, banks))):
@@ -143,17 +143,15 @@ def tile_rssmcell_pb_v_kernel(tc, h, embedding, wp1, bp1, wp2, bp2, wq1, bq1, wq
 
         def store1(staged, m, rows, first, count):
             view = out_1[P * m : P * (m + rows), COLS * first : COLS * (first + count)]
-            nc.sync.dma_start(out=view.rearrange("(r p) w -> p r w", p=P), in_=staged[:])
+            nc.sync.dma_start(out=view.rearrange("(r p) w -> p r w", p=P), in_=staged)
 
         v_raw = load("v_raw", rows4(vq), F32)
         g1_raw = load("g1_raw", rows4(grad_1), BF16)
         g0_raw = load("g0_raw", rows4(grad_0), BF16)
-        w2_raw = [load("w2_raw0", rows4(wq2[:, 0:COLS]), BF16)]
+        w2_raw = load("w2_raw", rows4(wq2), BF16)
         h_raw = load("h_raw", rows4(h), BF16)
-        z_raw = [load("z_raw0", rows4(zq[:, 0:COLS]), F32)]
-        w2_raw.append(load("w2_raw1", rows4(wq2[:, COLS:]), BF16))
+        z_raw = [load("z_raw%d" % pair, rows4(zq)[:, 2 * pair : 2 * pair + 2, :], F32) for pair in range(2)]
         e_raw = load("e_raw", rows4(embedding), BF16)
-        z_raw.append(load("z_raw1", rows4(zq[:, COLS:]), F32))
         w_raw = [load("w_raw%d" % g, rows4(wq1[COLS * g : COLS * (g + 1), DETER:]), BF16) for g in range(2)]
 
         ident = keep.tile([P, P], F32, name="ident")
@@ -179,7 +177,7 @@ def tile_rssmcell_pb_v_kernel(tc, h, embedding, wp1, bp1, wp2, bp2, wq1, bq1, wq
         banks = [transpose_pair(dz2, pair, s_free) for pair in range(2)]
         w2_grouped = [new_grouped()]
         for copy, cols in zip((vcopy, scopy), halves):
-            interleave_into(copy, w2_grouped[0][:, cols, :], w2_raw[0][:, :, cols])
+            interleave_into(copy, w2_grouped[0][:, cols, :], w2_raw[:, :, cols])
         dz2_grouped = new_grouped()
         for pair in range(2):
             gather_pair(scopy, dz2_grouped, pair, banks[pair])
@@ -187,13 +185,10 @@ def tile_rssmcell_pb_v_kernel(tc, h, embedding, wp1, bp1, wp2, bp2, wq1, bq1, wq
         for pair in range(2):
             quantize(dz2_op, dz2_grouped, E5M2, halves[pair])
         h_grouped = [interleave(scopy, chunk(h_raw, n)) for n in range(2)]
-        w2_grouped.append(interleave(scopy, w2_raw[1][:]))
 
         def w1_rows(n, g):
             return interleave(vcopy, chunk(w_raw[g], n))
 
-        def hid_gather(copy, g, pair, free):
-            gather_pair(copy, hid_grouped[g], pair, transpose_pair(dz1[g], pair, free))
 
         def out1_pair(staged, m, first, n):
             empty(scopy, staged, [(r, n - first) for r in range(2)], out1_banks([(m + r, n) for r in range(2)], s_free))
@@ -202,56 +197,62 @@ def tile_rssmcell_pb_v_kernel(tc, h, embedding, wp1, bp1, wp2, bp2, wq1, bq1, wq
             staged = new_staged(1, 5)
             empty(scopy, staged, [(0, n) for n in range(0, 2)], out1_banks([(m, n) for n in range(0, 2)], s_free))
             empty(scopy, staged, [(0, n) for n in range(2, 5)], out1_banks([(m, n) for n in range(2, 5)], s_free))
-            store1(staged, m, 1, 0, 5)
+            store1(staged[:], m, 1, 0, 5)
 
-        da = da_banks(0)
-        for j in range(PACK):
-            mask(0, j, da, halves[0])
+        da = [da_banks(0, v_free)]
+        w2_grouped.append(interleave(vcopy, chunk(w2_raw, 1)))
+        mask(0, 1, da[0])
+        mask(0, 0, da[0])
+        quantize(w2_op[1], w2_grouped[1], E4M3)
+        hid_grouped = [new_grouped()]
+        gather_pair(scopy, hid_grouped[0], 0, transpose_pair(dz1[0], 0, s_free))
+        da.append(da_banks(1, s_free))
         quantize(c_op[0], h_grouped[0], E4M3)
+        mask(0, 2, da[0], halves[0])
+        mask(0, 3, da[0], halves[0])
+        mask(0, 2, da[0], halves[1])
         tok_grouped = new_grouped()
         interleave_into(vcopy, tok_grouped[:, halves[0], :], dz1[0][:, :, halves[0]])
-        mask(0, 0, da, halves[1])
+        mask(0, 3, da[0], halves[1])
         quantize(dz1_tok[0], tok_grouped, E5M2, halves[0])
-        for j in range(1, PACK):
-            mask(0, j, da, halves[1])
         quantize(c_op[1], h_grouped[1], E4M3)
         interleave_into(vcopy, tok_grouped[:, halves[1], :], dz1[0][:, :, halves[1]])
         e_grouped = [interleave(vcopy, chunk(e_raw, 0))]
         quantize(dz1_tok[0], tok_grouped, E5M2, halves[1])
-        quantize(w2_op[1], w2_grouped[1], E4M3)
         quantize(c_op[2], e_grouped[0], E4M3)
-        hid_grouped = [new_grouped()]
         staged = new_staged(2, 2)
         for n in range(2):
             out1_pair(staged, 0, 0, n)
-        store1(staged, 0, 2, 0, 2)
-        for pair in range(2):
-            hid_gather(scopy, 0, pair, s_free)
+        store1(staged[:], 0, 2, 0, 2)
+        gather_pair(scopy, hid_grouped[0], 1, transpose_pair(dz1[0], 1, s_free))
         staged = new_staged(2, 2)
         for n in range(2):
             out1_pair(staged, 2, 0, n)
-        store1(staged, 2, 2, 0, 2)
-        da = da_banks(1)
-        e_grouped.append(interleave(vcopy, chunk(e_raw, 1)))
-        e_grouped.append(interleave(vcopy, chunk(e_raw, 2)))
-        quantize(c_op[3], e_grouped[1], E4M3)
-        quantize(c_op[4], e_grouped[2], E4M3)
-        for j in reversed(range(PACK)):
-            mask(1, j, da)
+        store1(staged[:], 2, 2, 0, 2)
+        for n in (1, 2):
+            e_grouped.append(interleave(vcopy, chunk(e_raw, n)))
+        for n in (1, 2):
+            quantize(c_op[2 + n], e_grouped[n], E4M3)
+        staged = new_staged(2, 3)
+        for n in range(2, 5):
+            out1_pair(staged, 0, 2, n)
+        for r in (1, 0):
+            store1(staged[:, r : r + 1, :], r, 1, 2, 3)
+        for j in (1, 0, 3, 2):
+            mask(1, j, da[1])
+        v_free.extend([s_free.pop(-4), s_free.pop(-3)])
+        held = transpose_pair(dz1[1], 0, v_free)
         quantize(dz1_hid[0], hid_grouped[0], E5M2)
         tok_grouped = interleave(vcopy, dz1[1][:])
         hid_grouped.append(new_grouped())
-        for m in (0, 2):
-            staged = new_staged(2, 3)
+        gather_pair(vcopy, hid_grouped[1], 0, held)
+        quantize(dz1_tok[1], tok_grouped, E5M2)
+        for m in (2, 3):
+            staged = new_staged(1, 3)
+            empty(scopy, staged, [(0, n) for n in range(3)], out1_banks([(m, 2 + n) for n in range(3)], s_free))
+            store1(staged[:], m, 1, 2, 3)
             if m == 2:
-                s_free.extend([v_free.pop(0), v_free.pop(0)])
-            for n in range(2, 5):
-                out1_pair(staged, m, 2, n)
-                if m == 2 and n == 3:
-                    hid_gather(vcopy, 1, 0, v_free)
-                    quantize(dz1_tok[1], tok_grouped, E5M2)
-                    hid_gather(vcopy, 1, 1, v_free)
-            store1(staged, m, 2, 2, 3)
+                gather_pair(vcopy, hid_grouped[1], 1, transpose_pair(dz1[1], 1, v_free))
 
         for n in range(3):
             w_grouped = [w1_rows(n, g) for g in range(2)]
@@ -259,14 +260,21 @@ def tile_rssmcell_pb_v_kernel(tc, h, embedding, wp1, bp1, wp2, bp2, wq1, bq1, wq
                 quantize(dz1_hid[1], hid_grouped[1], E5M2)
             for g in range(2):
                 quantize(w1_op[g][n], w_grouped[g], E4M3)
-        for m in range(4, 8):
-            out1_rows(m)
+        def out0_pair(copy, pair, n, free):
+            banks = out0_banks([(2 * pair + r, n) for r in range(2)], free)
+            return lambda: empty(copy, out0_staged[pair], [(r, n) for r in range(2)], banks)
 
+        for m in range(4, 7):
+            out1_rows(m)
+        early = out0_pair(vcopy, 1, 0, v_free)
+        out1_rows(7)
+
+        out0_staged = [new_staged(2, 3) for pair in range(2)]
+        early()
+        out0_pair(scopy, 0, 0, s_free)()
+        out0_pair(scopy, 0, 1, s_free)()
+        out0_pair(vcopy, 0, 2, s_free)()
+        out0_pair(scopy, 1, 1, v_free)()
+        out0_pair(vcopy, 1, 2, s_free)()
         for pair in range(2):
-            staged = new_staged(2, 3)
-            for n in range(3):
-                on_vector = n + pair >= 2
-                empty(vcopy if on_vector else scopy, staged, [(r, n) for r in range(2)], out0_banks([(2 * pair + r, n) for r in range(2)], v_free if on_vector else s_free))
-                if pair == 0 and n == 1:
-                    v_free.extend([s_free.pop(0), s_free.pop(0)])
-            nc.sync.dma_start(out=rows4(out_0)[:, 2 * pair : 2 * pair + 2, :], in_=staged[:])
+            nc.sync.dma_start(out=rows4(out_0)[:, 2 * pair : 2 * pair + 2, :], in_=out0_staged[pair][:])

@@ -23,6 +23,7 @@ P = 128
 PACK = 4
 COLS = 512
 HALF = COLS // 2
+DMA_ALIGN = 256
 
 
 def tile_rssmcell_pb_v_kernel(tc, h, embedding, wp1, bp1, wp2, bp2, wq1, bq1, wq2, bq2, zq, vq, grad_0, grad_1, grad_2, grad_3, out_0, out_1):
@@ -39,7 +40,7 @@ def tile_rssmcell_pb_v_kernel(tc, h, embedding, wp1, bp1, wp2, bp2, wq1, bq1, wq
             return ap.rearrange("(p j) w -> p j w", j=PACK)
 
         def load(name, view, dtype):
-            raw = keep.tile([P] + list(view.shape[1:]), dtype, name=name)
+            raw = keep.tile([P] + list(view.shape[1:]), dtype, name=name, align_bytes=DMA_ALIGN)
             nc.sync.dma_start(out=raw[:], in_=view)
             return raw
 
@@ -61,7 +62,7 @@ def tile_rssmcell_pb_v_kernel(tc, h, embedding, wp1, bp1, wp2, bp2, wq1, bq1, wq
             held[2].append(held[1])
 
         def new_staged(rows, count):
-            staged = staging.tile([P, rows, count * COLS], F32, name="staged")
+            staged = staging.tile([P, rows, count * COLS], F32, name="staged", align_bytes=DMA_ALIGN)
             return staged
 
         def chunk(raw, n):

@@ -120,8 +120,9 @@ def tile_rssmcell_pb_v_kernel(tc, h, embedding, wp1, bp1, wp2, bp2, wq1, bq1, wq
             if cols.stop == COLS:
                 s_free.append(banks[j][1])
 
-        def empty(copy, staged, places, banks):
-            for (r, at), bank in reversed(list(zip(places, banks))):
+        def empty(copy, staged, places, banks, last_first=True):
+            work = list(zip(places, banks))
+            for (r, at), bank in reversed(work) if last_first else work:
                 copy(out=staged[:, r, COLS * at : COLS * (at + 1)], in_=bank[0][:])
                 release(bank)
 
@@ -194,9 +195,9 @@ def tile_rssmcell_pb_v_kernel(tc, h, embedding, wp1, bp1, wp2, bp2, wq1, bq1, wq
         def out1_pair(staged, m, first, n):
             empty(scopy, staged, [(r, n - first) for r in range(2)], out1_banks([(m + r, n) for r in range(2)], s_free))
 
-        def out1_rows(m):
+        def out1_rows(m, copy=scopy, free=s_free):
             staged = new_staged(1, 5)
-            empty(scopy, staged, [(0, n) for n in range(0, 2)], out1_banks([(m, n) for n in range(0, 2)], s_free))
+            empty(copy, staged, [(0, n) for n in range(0, 2)], out1_banks([(m, n) for n in range(0, 2)], free))
             empty(scopy, staged, [(0, n) for n in range(2, 5)], out1_banks([(m, n) for n in range(2, 5)], s_free))
             store1(staged[:], m, 1, 0, 5)
 
@@ -217,19 +218,20 @@ def tile_rssmcell_pb_v_kernel(tc, h, embedding, wp1, bp1, wp2, bp2, wq1, bq1, wq
         mask(0, 3, da[0], halves[1])
         quantize(dz1_tok[0], tok_grouped, E5M2, halves[0])
         quantize(c_op[1], h_grouped[1], E4M3)
-        interleave_into(vcopy, tok_grouped[:, halves[1], :], dz1[0][:, :, halves[1]])
+        interleave_into(scopy, tok_grouped[:, halves[1], :], dz1[0][:, :, halves[1]])
+        mask(1, 1, da[1])
         e_grouped = [interleave(vcopy, chunk(e_raw, 0))]
         quantize(dz1_tok[0], tok_grouped, E5M2, halves[1])
         quantize(c_op[2], e_grouped[0], E4M3)
-        staged = new_staged(2, 2)
-        for n in range(2):
-            out1_pair(staged, 0, 0, n)
-        store1(staged[:], 0, 2, 0, 2)
-        gather_pair(scopy, hid_grouped[0], 1, transpose_pair(dz1[0], 1, s_free))
-        staged = new_staged(2, 2)
-        for n in range(2):
-            out1_pair(staged, 2, 0, n)
-        store1(staged[:], 2, 2, 0, 2)
+        v_free.append(s_free.pop())
+        for m in (0, 2):
+            staged = new_staged(2, 2)
+            for n in range(2):
+                out1_pair(staged, m, 0, n)
+            for r in (1, 0):
+                store1(staged[:, r : r + 1, :], m + r, 1, 0, 2)
+            if m == 0:
+                gather_pair(scopy, hid_grouped[0], 1, transpose_pair(dz1[0], 1, s_free))
         for n in (1, 2):
             e_grouped.append(interleave(vcopy, chunk(e_raw, n)))
         for n in (1, 2):
@@ -239,43 +241,46 @@ def tile_rssmcell_pb_v_kernel(tc, h, embedding, wp1, bp1, wp2, bp2, wq1, bq1, wq
             out1_pair(staged, 0, 2, n)
         for r in (1, 0):
             store1(staged[:, r : r + 1, :], r, 1, 2, 3)
-        for j in (1, 0, 3, 2):
+        for j in (0, 3, 2):
             mask(1, j, da[1])
-        v_free.extend([s_free.pop(-4), s_free.pop(-3)])
-        held = transpose_pair(dz1[1], 0, v_free)
+        v_free.append(s_free.pop(-3))
         quantize(dz1_hid[0], hid_grouped[0], E5M2)
         tok_grouped = interleave(vcopy, dz1[1][:])
         hid_grouped.append(new_grouped())
-        gather_pair(vcopy, hid_grouped[1], 0, held)
-        quantize(dz1_tok[1], tok_grouped, E5M2)
         for m in (2, 3):
+            gather_pair(vcopy, hid_grouped[1], m - 2, transpose_pair(dz1[1], m - 2, v_free))
             staged = new_staged(1, 3)
             empty(scopy, staged, [(0, n) for n in range(3)], out1_banks([(m, 2 + n) for n in range(3)], s_free))
             store1(staged[:], m, 1, 2, 3)
             if m == 2:
-                gather_pair(vcopy, hid_grouped[1], 1, transpose_pair(dz1[1], 1, v_free))
+                quantize(dz1_tok[1], tok_grouped, E5M2)
 
-        for n in range(3):
-            w_grouped = [w1_rows(n, g) for g in range(2)]
-            if n == 0:
-                quantize(dz1_hid[1], hid_grouped[1], E5M2)
-            for g in range(2):
-                quantize(w1_op[g][n], w_grouped[g], E4M3)
-        def out0_pair(copy, pair, n, free):
+        w_grouped = [w1_rows(0, 0)]
+        out1_rows(4, vcopy, v_free)
+        quantize(w1_op[0][0], w_grouped[0], E4M3)
+        w_grouped.append(w1_rows(0, 1))
+        quantize(dz1_hid[1], hid_grouped[1], E5M2)
+        for step in range(1, 6):
+            if step < 5:
+                w_grouped.append(w1_rows((step + 1) // 2, (step + 1) % 2))
+            quantize(w1_op[step % 2][step // 2], w_grouped[step], E4M3)
+
+        def out0_pair(copy, pair, n, free, last_first=True):
             banks = out0_banks([(2 * pair + r, n) for r in range(2)], free)
-            return lambda: empty(copy, out0_staged[pair], [(r, n) for r in range(2)], banks)
+            return lambda: empty(copy, out0_staged[pair], [(r, n) for r in range(2)], banks, last_first)
 
-        for m in range(4, 7):
-            out1_rows(m)
+        out1_rows(5)
+        out1_rows(6)
         early = out0_pair(vcopy, 1, 0, v_free)
         out1_rows(7)
 
         out0_staged = [new_staged(2, 3) for pair in range(2)]
-        early()
         out0_pair(scopy, 0, 0, s_free)()
         out0_pair(scopy, 0, 1, s_free)()
-        out0_pair(vcopy, 0, 2, s_free)()
-        out0_pair(scopy, 1, 1, v_free)()
-        out0_pair(vcopy, 1, 2, s_free)()
+        late = out0_pair(scopy, 1, 1, s_free)
+        early()
+        out0_pair(vcopy, 0, 2, s_free, False)()
+        late()
+        out0_pair(vcopy, 1, 2, s_free, False)()
         for pair in range(2):
             nc.sync.dma_start(out=rows4(out_0)[:, 2 * pair : 2 * pair + 2, :], in_=out0_staged[pair][:])

@@ -80,15 +80,19 @@ def tile_rssmcell_pb_v_kernel(tc, h, embedding, wp1, bp1, wp2, bp2, wq1, bq1, wq
             codes, scales = target
             nc.vector.quantize_mx(out=codes[:, cols].bitcast(fmt), scales=scales[:, cols], in_=grouped[:, cols, :].rearrange("p w t -> p (w t)"))
 
-        def transpose_pair(rows, pair, free):
+        def transpose_pair(words_of, pair, free):
             held = new_bank(free)
-            bank = held[0]
             for jj in range(2):
-                words = rows[:, 2 * pair + jj, :].bitcast(F32)
                 for u in range(2):
                     at = P * (2 * jj + u)
-                    nc.tensor.transpose(bank[:, at : at + P], words[:, u::2], ident[:])
+                    nc.tensor.transpose(held[0][:, at : at + P], words_of(2 * pair + jj, u), ident[:])
             return held
+
+        def dz2_words(j, u):
+            return dz2[:, u, j, :].bitcast(F32)
+
+        def dz1_words(g):
+            return lambda j, u: dz1[g][:, j, :].bitcast(F32)[:, u::2]
 
         def gather_pair(copy, grouped, pair, held):
             words = grouped[:].rearrange("p w t -> p (w t)").bitcast(F32)
@@ -107,9 +111,9 @@ def tile_rssmcell_pb_v_kernel(tc, h, embedding, wp1, bp1, wp2, bp2, wq1, bq1, wq
                 stop=stop,
             )
 
-        def da_banks(g, free):
+        def da_banks(g, free, js):
             banks = []
-            for j in range(PACK):
+            for j in js:
                 bank = new_bank(free)
                 mx(bank, dz2_op, j, w2_op[g], True, True)
                 banks.append(bank)
@@ -148,12 +152,12 @@ def tile_rssmcell_pb_v_kernel(tc, h, embedding, wp1, bp1, wp2, bp2, wq1, bq1, wq
             nc.sync.dma_start(out=view.rearrange("(r p) w -> p r w", p=P), in_=staged)
 
         v_raw = load("v_raw", rows4(vq), F32)
+        e_raw = load("e_raw", rows4(embedding), BF16)
         g1_raw = load("g1_raw", rows4(grad_1), BF16)
         g0_raw = load("g0_raw", rows4(grad_0), BF16)
         w2_raw = load("w2_raw", rows4(wq2), BF16)
         h_raw = load("h_raw", rows4(h), BF16)
         z_raw = [load("z_raw%d" % pair, rows4(zq)[:, 2 * pair : 2 * pair + 2, :], F32) for pair in range(2)]
-        e_raw = load("e_raw", rows4(embedding), BF16)
         w_raw = [load("w_raw%d" % g, rows4(wq1[COLS * g : COLS * (g + 1), DETER:]), BF16) for g in range(2)]
 
         ident = keep.tile([P, P], F32, name="ident")
@@ -166,110 +170,110 @@ def tile_rssmcell_pb_v_kernel(tc, h, embedding, wp1, bp1, wp2, bp2, wq1, bq1, wq
         c_op = [operand("c%d" % n) for n in range(5)]
         w1_op = [[operand("w1_%d_%d" % (g, n)) for n in range(3)] for g in range(2)]
         dz1 = [keep.tile([P, PACK, COLS], BF16, name="dz1_%d" % g) for g in range(2)]
-        dz2 = keep.tile([P, PACK, DIST], BF16, name="dz2")
+        dz2 = keep.tile([P, 2, PACK, STOC], BF16, name="dz2")
         sig = keep.tile([P, PACK, STOC], F32, name="sig")
         s_free, v_free = [0, 1, 2, 3], [4, 5, 6, 7]
         halves = (slice(0, HALF), slice(HALF, COLS))
 
-        for pair in range(2):
-            js = slice(2 * pair, 2 * pair + 2)
-            nc.scalar.activation(out=sig[:, js, :], in_=v_raw[:, js, :], func=SIGMOID)
-            nc.vector.tensor_tensor(out=dz2[:, js, STOC:], in0=g1_raw[:, js, :], in1=sig[:, js, :], op=MULT)
-        scopy(out=dz2[:, :, 0:STOC], in_=g0_raw[:])
-        banks = [transpose_pair(dz2, pair, s_free) for pair in range(2)]
-        w2_grouped = [new_grouped()]
-        for copy, cols in zip((vcopy, scopy), halves):
-            interleave_into(copy, w2_grouped[0][:, cols, :], w2_raw[:, :, cols])
-        dz2_grouped = new_grouped()
-        for pair in range(2):
-            gather_pair(scopy, dz2_grouped, pair, banks[pair])
-        quantize(w2_op[0], w2_grouped[0], E4M3)
-        for pair in range(2):
-            quantize(dz2_op, dz2_grouped, E5M2, halves[pair])
-        h_grouped = [interleave(scopy, chunk(h_raw, n)) for n in range(2)]
-
         def w1_rows(n, g):
             return interleave(vcopy, chunk(w_raw[g], n))
 
-
-        def out1_pair(staged, m, first, n):
-            empty(scopy, staged, [(r, n - first) for r in range(2)], out1_banks([(m + r, n) for r in range(2)], s_free))
+        def out1_part(copy, staged, m, ns, free, last_first=True):
+            banks = out1_banks([(m, n) for n in ns], free)
+            return lambda: empty(copy, staged, [(0, n) for n in ns], banks, last_first)
 
         def out1_rows(m, copy=scopy, free=s_free):
             staged = new_staged(1, 5)
-            empty(copy, staged, [(0, n) for n in range(0, 2)], out1_banks([(m, n) for n in range(0, 2)], free))
-            empty(scopy, staged, [(0, n) for n in range(2, 5)], out1_banks([(m, n) for n in range(2, 5)], s_free))
+            out1_part(scopy, staged, m, (2, 3, 4), s_free)()
+            out1_part(copy, staged, m, (0, 1), free)()
             store1(staged[:], m, 1, 0, 5)
 
-        da = [da_banks(0, v_free)]
-        w2_grouped.append(interleave(vcopy, chunk(w2_raw, 1)))
-        mask(0, 1, da[0])
-        mask(0, 0, da[0])
+        def out0_pair(copy, pair, n, free, last_first=True):
+            banks = out0_banks([(2 * pair + r, n) for r in range(2)], free)
+            return lambda: empty(copy, out0_staged[pair], [(r, n) for r in range(2)], banks, last_first)
+
+        nc.scalar.activation(out=sig[:], in_=v_raw[:], func=SIGMOID)
+        e_grouped = [interleave(vcopy, chunk(e_raw, 0)), new_grouped(), new_grouped()]
+        interleave_into(scopy, e_grouped[2][:, halves[0], :], chunk(e_raw, 2)[:, :, halves[0]])
+
+        for pair in range(2):
+            js = slice(2 * pair, 2 * pair + 2)
+            nc.vector.tensor_tensor(
+                out=dz2[:, :, js, P:].rearrange("p u j (w e) -> p u j w e", e=2),
+                in0=g1_raw[:, js, :].rearrange("p j (w u e) -> p u j w e", u=2, e=2),
+                in1=sig[:, js, :].rearrange("p j (w u e) -> p u j w e", u=2, e=2),
+                op=MULT,
+            )
+        scopy(out=dz2[:, :, :, 0:P].bitcast(F32), in_=g0_raw[:].bitcast(F32).rearrange("p j (w u) -> p u j w", u=2))
+        interleave_into(scopy, e_grouped[2][:, halves[1], :], chunk(e_raw, 2)[:, :, halves[1]])
+        banks = [transpose_pair(dz2_words, pair, s_free) for pair in range(2)]
+        interleave_into(vcopy, e_grouped[1][:], chunk(e_raw, 1))
+        w2_grouped = [interleave(vcopy, chunk(w2_raw, 0))]
+        quantize(c_op[2], e_grouped[0], E4M3)
+        dz2_grouped = new_grouped()
+        for pair in range(2):
+            gather_pair(scopy, dz2_grouped, pair, banks[pair])
+        quantize(dz2_op, dz2_grouped, E5M2)
+        quantize(w2_op[0], w2_grouped[0], E4M3)
+        quantize(c_op[3], e_grouped[1], E4M3)
+        quantize(c_op[4], e_grouped[2], E4M3)
+        w2_grouped.append(interleave(scopy, chunk(w2_raw, 1)))
+        h_grouped = [interleave(scopy, chunk(h_raw, n)) for n in range(2)]
+
+        da = [da_banks(0, v_free, range(PACK))]
         quantize(w2_op[1], w2_grouped[1], E4M3)
-        hid_grouped = [new_grouped()]
-        gather_pair(scopy, hid_grouped[0], 0, transpose_pair(dz1[0], 0, s_free))
-        da.append(da_banks(1, s_free))
+        mask(0, 0, da[0])
+        mask(0, 1, da[0])
+        da.append(da_banks(1, s_free, (0,)))
         quantize(c_op[0], h_grouped[0], E4M3)
+        hid_grouped = [new_grouped()]
+        held = transpose_pair(dz1_words(0), 0, s_free)
         mask(0, 2, da[0], halves[0])
         mask(0, 3, da[0], halves[0])
         mask(0, 2, da[0], halves[1])
+        gather_pair(scopy, hid_grouped[0], 0, held)
+        s_free.insert(0, s_free.pop(-2))
+        da[1].extend(da_banks(1, s_free, (1, 2, 3)))
         tok_grouped = new_grouped()
         interleave_into(vcopy, tok_grouped[:, halves[0], :], dz1[0][:, :, halves[0]])
         mask(0, 3, da[0], halves[1])
         quantize(dz1_tok[0], tok_grouped, E5M2, halves[0])
         quantize(c_op[1], h_grouped[1], E4M3)
         interleave_into(scopy, tok_grouped[:, halves[1], :], dz1[0][:, :, halves[1]])
-        mask(1, 1, da[1])
-        e_grouped = [interleave(vcopy, chunk(e_raw, 0))]
-        quantize(dz1_tok[0], tok_grouped, E5M2, halves[1])
-        quantize(c_op[2], e_grouped[0], E4M3)
-        v_free.append(s_free.pop())
-        for m in (0, 2):
-            staged = new_staged(2, 2)
-            for n in range(2):
-                out1_pair(staged, m, 0, n)
-            for r in (1, 0):
-                store1(staged[:, r : r + 1, :], m + r, 1, 0, 2)
+        mask(1, 0, da[1])
+        for m in range(2):
+            staged = new_staged(1, 5)
+            for n, copy in ((3, vcopy), (4, scopy), (2, vcopy), (0, scopy), (1, scopy)):
+                out1_part(copy, staged, m, (n,), s_free)()
             if m == 0:
-                gather_pair(scopy, hid_grouped[0], 1, transpose_pair(dz1[0], 1, s_free))
-        for n in (1, 2):
-            e_grouped.append(interleave(vcopy, chunk(e_raw, n)))
-        for n in (1, 2):
-            quantize(c_op[2 + n], e_grouped[n], E4M3)
-        staged = new_staged(2, 3)
-        for n in range(2, 5):
-            out1_pair(staged, 0, 2, n)
-        for r in (1, 0):
-            store1(staged[:, r : r + 1, :], r, 1, 2, 3)
-        for j in (0, 3, 2):
+                store1(staged[:, :, 3 * COLS :], m, 1, 3, 2)
+                store1(staged[:, :, 0 : 3 * COLS], m, 1, 0, 3)
+                quantize(dz1_tok[0], tok_grouped, E5M2, halves[1])
+            else:
+                store1(staged[:], m, 1, 0, 5)
+        for j in (1, 3, 2):
             mask(1, j, da[1])
-        v_free.append(s_free.pop(-3))
-        quantize(dz1_hid[0], hid_grouped[0], E5M2)
-        tok_grouped = interleave(vcopy, dz1[1][:])
-        hid_grouped.append(new_grouped())
-        for m in (2, 3):
-            gather_pair(vcopy, hid_grouped[1], m - 2, transpose_pair(dz1[1], m - 2, v_free))
-            staged = new_staged(1, 3)
-            empty(scopy, staged, [(0, n) for n in range(3)], out1_banks([(m, 2 + n) for n in range(3)], s_free))
-            store1(staged[:], m, 1, 2, 3)
-            if m == 2:
-                quantize(dz1_tok[1], tok_grouped, E5M2)
-
+        v_free.extend([s_free.pop(-3), s_free.pop(-2)])
+        out1_rows(2)
         w_grouped = [w1_rows(0, 0)]
-        out1_rows(4, vcopy, v_free)
+        tok_grouped = interleave(vcopy, dz1[1][:])
+        gather_pair(vcopy, hid_grouped[0], 1, transpose_pair(dz1_words(0), 1, v_free))
+        quantize(dz1_tok[1], tok_grouped, E5M2)
+        hid_grouped.append(new_grouped())
+        out1_rows(3)
+        gather_pair(vcopy, hid_grouped[1], 0, transpose_pair(dz1_words(1), 0, v_free))
+        quantize(dz1_hid[0], hid_grouped[0], E5M2)
         quantize(w1_op[0][0], w_grouped[0], E4M3)
+        out1_rows(4, vcopy, v_free)
         w_grouped.append(w1_rows(0, 1))
-        quantize(dz1_hid[1], hid_grouped[1], E5M2)
+        gather_pair(scopy, hid_grouped[1], 1, transpose_pair(dz1_words(1), 1, s_free))
+        out1_rows(5)
         for step in range(1, 6):
             if step < 5:
                 w_grouped.append(w1_rows((step + 1) // 2, (step + 1) % 2))
             quantize(w1_op[step % 2][step // 2], w_grouped[step], E4M3)
-
-        def out0_pair(copy, pair, n, free, last_first=True):
-            banks = out0_banks([(2 * pair + r, n) for r in range(2)], free)
-            return lambda: empty(copy, out0_staged[pair], [(r, n) for r in range(2)], banks, last_first)
-
-        out1_rows(5)
+            if step == 1:
+                quantize(dz1_hid[1], hid_grouped[1], E5M2)
         out1_rows(6)
         early = out0_pair(vcopy, 1, 0, v_free)
         out1_rows(7)

@@ -158,7 +158,12 @@ def tile_rssmcell_pb_v_kernel(tc, h, embedding, wp1, bp1, wp2, bp2, wq1, bq1, wq
         w2_raw = load("w2_raw", rows4(wq2), BF16)
         h_raw = load("h_raw", rows4(h), BF16)
         z_raw = [load("z_raw%d" % pair, rows4(zq)[:, 2 * pair : 2 * pair + 2, :], F32) for pair in range(2)]
-        w_raw = [load("w_raw%d" % g, rows4(wq1[COLS * g : COLS * (g + 1), DETER:]), BF16) for g in range(2)]
+        w_raw = []
+        for g in range(2):
+            raw = keep.tile([P, PACK, EMBED], BF16, name="w_raw%d" % g, align_bytes=DMA_ALIGN)
+            for js in (slice(0, 2), slice(2, 3), slice(3, 4)):
+                nc.sync.dma_start(out=raw[:, js, :], in_=rows4(wq1[COLS * g : COLS * (g + 1), DETER:])[:, js, :])
+            w_raw.append(raw)
 
         ident = keep.tile([P, P], F32, name="ident")
         make_identity(nc, ident[:])
@@ -233,28 +238,30 @@ def tile_rssmcell_pb_v_kernel(tc, h, embedding, wp1, bp1, wp2, bp2, wq1, bq1, wq
         mask(0, 2, da[0], halves[1])
         gather_pair(scopy, hid_grouped[0], 0, held)
         s_free.insert(0, s_free.pop(-2))
-        da[1].extend(da_banks(1, s_free, (1, 2, 3)))
+        da[1].extend(da_banks(1, s_free, (1, 2)))
         tok_grouped = new_grouped()
         interleave_into(vcopy, tok_grouped[:, halves[0], :], dz1[0][:, :, halves[0]])
         mask(0, 3, da[0], halves[1])
         quantize(dz1_tok[0], tok_grouped, E5M2, halves[0])
         quantize(c_op[1], h_grouped[1], E4M3)
         interleave_into(scopy, tok_grouped[:, halves[1], :], dz1[0][:, :, halves[1]])
-        mask(1, 0, da[1])
         for m in range(2):
             staged = new_staged(1, 5)
-            for n, copy in ((3, vcopy), (4, scopy), (2, vcopy), (0, scopy), (1, scopy)):
+            for n, copy in ((3, scopy if m else vcopy), (4, scopy), (2, vcopy), (0, scopy), (1, scopy if m else vcopy)):
                 out1_part(copy, staged, m, (n,), s_free)()
+            store1(staged[:], m, 1, 0, 5)
             if m == 0:
-                store1(staged[:, :, 3 * COLS :], m, 1, 3, 2)
-                store1(staged[:, :, 0 : 3 * COLS], m, 1, 0, 3)
                 quantize(dz1_tok[0], tok_grouped, E5M2, halves[1])
-            else:
-                store1(staged[:], m, 1, 0, 5)
-        for j in (1, 3, 2):
+                mask(1, 0, da[1])
+        staged = new_staged(1, 5)
+        out1_part(scopy, staged, 2, (0, 1), s_free)()
+        da[1].extend(da_banks(1, s_free, (3,)))
+        for j in (1, 2):
             mask(1, j, da[1])
-        v_free.extend([s_free.pop(-3), s_free.pop(-2)])
-        out1_rows(2)
+        out1_part(scopy, staged, 2, (2, 3, 4), s_free)()
+        store1(staged[:], 2, 1, 0, 5)
+        mask(1, 3, da[1])
+        v_free.extend([s_free.pop(0), s_free.pop()])
         w_grouped = [w1_rows(0, 0)]
         tok_grouped = interleave(vcopy, dz1[1][:])
         gather_pair(vcopy, hid_grouped[0], 1, transpose_pair(dz1_words(0), 1, v_free))

@@ -152,9 +152,9 @@ def tile_rssmcell_pb_v_kernel(tc, h, embedding, wp1, bp1, wp2, bp2, wq1, bq1, wq
             nc.sync.dma_start(out=view.rearrange("(r p) w -> p r w", p=P), in_=staged)
 
         v_raw = load("v_raw", rows4(vq), F32)
-        e_raw = load("e_raw", rows4(embedding), BF16)
         g1_raw = load("g1_raw", rows4(grad_1), BF16)
         g0_raw = load("g0_raw", rows4(grad_0), BF16)
+        e_raw = load("e_raw", rows4(embedding), BF16)
         w2_raw = load("w2_raw", rows4(wq2), BF16)
         h_raw = load("h_raw", rows4(h), BF16)
         z_raw = [load("z_raw%d" % pair, rows4(zq)[:, 2 * pair : 2 * pair + 2, :], F32) for pair in range(2)]
@@ -197,12 +197,9 @@ def tile_rssmcell_pb_v_kernel(tc, h, embedding, wp1, bp1, wp2, bp2, wq1, bq1, wq
             banks = out0_banks([(2 * pair + r, n) for r in range(2)], free)
             return lambda: empty(copy, out0_staged[pair], [(r, n) for r in range(2)], banks, last_first)
 
-        nc.scalar.activation(out=sig[:], in_=v_raw[:], func=SIGMOID)
-        e_grouped = [interleave(vcopy, chunk(e_raw, 0)), new_grouped(), new_grouped()]
-        interleave_into(scopy, e_grouped[2][:, halves[0], :], chunk(e_raw, 2)[:, :, halves[0]])
-
         for pair in range(2):
             js = slice(2 * pair, 2 * pair + 2)
+            nc.scalar.activation(out=sig[:, js, :], in_=v_raw[:, js, :], func=SIGMOID)
             nc.vector.tensor_tensor(
                 out=dz2[:, :, js, P:].rearrange("p u j (w e) -> p u j w e", e=2),
                 in0=g1_raw[:, js, :].rearrange("p j (w u e) -> p u j w e", u=2, e=2),
@@ -210,45 +207,53 @@ def tile_rssmcell_pb_v_kernel(tc, h, embedding, wp1, bp1, wp2, bp2, wq1, bq1, wq
                 op=MULT,
             )
         scopy(out=dz2[:, :, :, 0:P].bitcast(F32), in_=g0_raw[:].bitcast(F32).rearrange("p j (w u) -> p u j w", u=2))
-        interleave_into(scopy, e_grouped[2][:, halves[1], :], chunk(e_raw, 2)[:, :, halves[1]])
         banks = [transpose_pair(dz2_words, pair, s_free) for pair in range(2)]
-        interleave_into(vcopy, e_grouped[1][:], chunk(e_raw, 1))
-        w2_grouped = [interleave(vcopy, chunk(w2_raw, 0))]
-        quantize(c_op[2], e_grouped[0], E4M3)
         dz2_grouped = new_grouped()
         for pair in range(2):
             gather_pair(scopy, dz2_grouped, pair, banks[pair])
+
+        e_grouped = [interleave(vcopy, chunk(e_raw, 0)), new_grouped()]
         quantize(dz2_op, dz2_grouped, E5M2)
-        quantize(w2_op[0], w2_grouped[0], E4M3)
+        for copy, cols in zip((vcopy, scopy), halves):
+            interleave_into(copy, e_grouped[1][:, cols, :], chunk(e_raw, 1)[:, :, cols])
+        quantize(c_op[2], e_grouped[0], E4M3)
+        e_grouped.append(interleave(scopy, chunk(e_raw, 2)))
+        w2_grouped = [interleave(copy, chunk(w2_raw, n)) for n, copy in enumerate((vcopy, scopy))]
         quantize(c_op[3], e_grouped[1], E4M3)
+        quantize(w2_op[0], w2_grouped[0], E4M3)
         quantize(c_op[4], e_grouped[2], E4M3)
-        w2_grouped.append(interleave(scopy, chunk(w2_raw, 1)))
         h_grouped = [interleave(scopy, chunk(h_raw, n)) for n in range(2)]
 
         da = [da_banks(0, v_free, range(PACK))]
         quantize(w2_op[1], w2_grouped[1], E4M3)
         mask(0, 0, da[0])
         mask(0, 1, da[0])
+        s_free.insert(0, s_free.pop())
         da.append(da_banks(1, s_free, (0,)))
         quantize(c_op[0], h_grouped[0], E4M3)
         hid_grouped = [new_grouped()]
         held = transpose_pair(dz1_words(0), 0, s_free)
-        mask(0, 2, da[0], halves[0])
-        mask(0, 3, da[0], halves[0])
-        mask(0, 2, da[0], halves[1])
+        da[1].extend(da_banks(1, s_free, (1,)))
+        first, second, rest = slice(0, P), slice(P, HALF), slice(P, COLS)
+        mask(0, 2, da[0], first)
+        mask(0, 3, da[0], first)
+        mask(0, 2, da[0], rest)
         gather_pair(scopy, hid_grouped[0], 0, held)
         s_free.insert(0, s_free.pop(-2))
-        da[1].extend(da_banks(1, s_free, (1, 2)))
+        da[1].extend(da_banks(1, s_free, (2,)))
         tok_grouped = new_grouped()
-        interleave_into(vcopy, tok_grouped[:, halves[0], :], dz1[0][:, :, halves[0]])
-        mask(0, 3, da[0], halves[1])
-        quantize(dz1_tok[0], tok_grouped, E5M2, halves[0])
+        interleave_into(vcopy, tok_grouped[:, first, :], dz1[0][:, :, first])
+        mask(0, 3, da[0], rest)
+        quantize(dz1_tok[0], tok_grouped, E5M2, first)
         quantize(c_op[1], h_grouped[1], E4M3)
+        interleave_into(vcopy, tok_grouped[:, second, :], dz1[0][:, :, second])
         interleave_into(scopy, tok_grouped[:, halves[1], :], dz1[0][:, :, halves[1]])
         for m in range(2):
             staged = new_staged(1, 5)
             for n, copy in ((3, scopy if m else vcopy), (4, scopy), (2, vcopy), (0, scopy), (1, scopy if m else vcopy)):
                 out1_part(copy, staged, m, (n,), s_free)()
+                if m == 0 and n == 3:
+                    quantize(dz1_tok[0], tok_grouped, E5M2, second)
             store1(staged[:], m, 1, 0, 5)
             if m == 0:
                 quantize(dz1_tok[0], tok_grouped, E5M2, halves[1])
@@ -262,13 +267,15 @@ def tile_rssmcell_pb_v_kernel(tc, h, embedding, wp1, bp1, wp2, bp2, wq1, bq1, wq
         store1(staged[:], 2, 1, 0, 5)
         mask(1, 3, da[1])
         v_free.extend([s_free.pop(0), s_free.pop()])
-        w_grouped = [w1_rows(0, 0)]
+        w_grouped = [new_grouped()]
+        interleave_into(vcopy, w_grouped[0][:, halves[0], :], chunk(w_raw[0], 0)[:, :, halves[0]])
         tok_grouped = interleave(vcopy, dz1[1][:])
         gather_pair(vcopy, hid_grouped[0], 1, transpose_pair(dz1_words(0), 1, v_free))
         quantize(dz1_tok[1], tok_grouped, E5M2)
         hid_grouped.append(new_grouped())
         out1_rows(3)
         gather_pair(vcopy, hid_grouped[1], 0, transpose_pair(dz1_words(1), 0, v_free))
+        interleave_into(vcopy, w_grouped[0][:, halves[1], :], chunk(w_raw[0], 0)[:, :, halves[1]])
         quantize(dz1_hid[0], hid_grouped[0], E5M2)
         quantize(w1_op[0][0], w_grouped[0], E4M3)
         out1_rows(4, vcopy, v_free)

@@ -247,17 +247,18 @@ def tile_rssmcell_pb_v_kernel(tc, h, embedding, wp1, bp1, wp2, bp2, wq1, bq1, wq
         quantize(dz1_tok[0], tok_grouped, E5M2, first)
         quantize(c_op[1], h_grouped[1], E4M3)
         interleave_into(vcopy, tok_grouped[:, second, :], dz1[0][:, :, second])
-        interleave_into(scopy, tok_grouped[:, halves[1], :], dz1[0][:, :, halves[1]])
+        third, fourth = slice(HALF, HALF + P), slice(HALF + P, COLS)
+        interleave_into(scopy, tok_grouped[:, third, :], dz1[0][:, :, third])
+        quantize(dz1_tok[0], tok_grouped, E5M2, second)
         for m in range(2):
             staged = new_staged(1, 5)
-            for n, copy in ((3, scopy if m else vcopy), (4, scopy), (2, vcopy), (0, scopy), (1, scopy if m else vcopy)):
+            for n, copy in ((3, scopy), (4, scopy if m else vcopy), (2, vcopy if m else scopy), (0, scopy if m else vcopy), (1, scopy)):
                 out1_part(copy, staged, m, (n,), s_free)()
-                if m == 0 and n == 3:
-                    quantize(dz1_tok[0], tok_grouped, E5M2, second)
             store1(staged[:], m, 1, 0, 5)
             if m == 0:
-                quantize(dz1_tok[0], tok_grouped, E5M2, halves[1])
+                interleave_into(vcopy, tok_grouped[:, fourth, :], dz1[0][:, :, fourth])
                 mask(1, 0, da[1])
+                quantize(dz1_tok[0], tok_grouped, E5M2, halves[1])
         staged = new_staged(1, 5)
         out1_part(scopy, staged, 2, (0, 1), s_free)()
         da[1].extend(da_banks(1, s_free, (3,)))

@@ -39,9 +39,9 @@ def tile_rssmcell_pb_v_kernel(tc, h, embedding, wp1, bp1, wp2, bp2, wq1, bq1, wq
         def rows4(ap):
             return ap.rearrange("(p j) w -> p j w", j=PACK)
 
-        def load(name, view, dtype):
+        def load(name, view, dtype, queue=nc.sync):
             raw = keep.tile([P] + list(view.shape[1:]), dtype, name=name, align_bytes=DMA_ALIGN)
-            nc.sync.dma_start(out=raw[:], in_=view)
+            queue.dma_start(out=raw[:], in_=view)
             return raw
 
         def operand(name):
@@ -151,7 +151,7 @@ def tile_rssmcell_pb_v_kernel(tc, h, embedding, wp1, bp1, wp2, bp2, wq1, bq1, wq
             view = out_1[P * m : P * (m + rows), COLS * first : COLS * (first + count)]
             nc.sync.dma_start(out=view.rearrange("(r p) w -> p r w", p=P), in_=staged)
 
-        v_raw = load("v_raw", rows4(vq), F32)
+        v_raw = load("v_raw", rows4(vq), F32, nc.scalar)
         g1_raw = load("g1_raw", rows4(grad_1), BF16)
         g0_raw = load("g0_raw", rows4(grad_0), BF16)
         e_raw = load("e_raw", rows4(embedding), BF16)

@@ -149,7 +149,7 @@ def tile_rssmcell_pb_v_kernel(tc, h, embedding, wp1, bp1, wp2, bp2, wq1, bq1, wq
 
         def store1(staged, m, rows, first, count):
             view = out_1[P * m : P * (m + rows), COLS * first : COLS * (first + count)]
-            nc.sync.dma_start(out=view.rearrange("(r p) w -> p r w", p=P), in_=staged)
+            nc.sync.dma_start(out=view.rearrange("(r p) w -> p r w", p=P), in_=staged, max_dma_last_dim=2560)
 
         v_raw = load("v_raw", rows4(vq), F32, nc.scalar)
         g1_raw = load("g1_raw", rows4(grad_1), BF16)

@@ -5,9 +5,10 @@ from concourse.masks import make_identity
 
 B, EMBED, DETER, STOC, HID = 512, 1536, 1024, 256, 1024
 DIST = 2 * STOC
+CAT = DETER + EMBED
 
-FLOPS = 2 * (B * DIST * HID + B * HID * EMBED + HID * B * (DETER + EMBED))
-BYTES = 2 * (2 * B * STOC + DIST * HID + HID * EMBED + B * (DETER + EMBED)) + 4 * (B * STOC + B * HID) + 4 * (B * EMBED + HID * (DETER + EMBED))
+FLOPS = 2 * (B * DIST * HID + B * HID * EMBED + HID * B * CAT)
+BYTES = 2 * (2 * B * STOC + DIST * HID + HID * EMBED + B * CAT) + 4 * (B * STOC + B * HID) + 4 * (B * EMBED + HID * CAT)
 
 F32 = mybir.dt.float32
 BF16 = mybir.dt.bfloat16
@@ -24,14 +25,16 @@ PACK = 4
 COLS = 512
 HALF = COLS // 2
 DMA_ALIGN = 256
+KIB = 1024
+GROUPS = (1, 1, 2, 2, 2)
 
 
 def tile_rssmcell_pb_v_kernel(tc, h, embedding, wp1, bp1, wp2, bp2, wq1, bq1, wq2, bq2, zq, vq, grad_0, grad_1, grad_2, grad_3, out_0, out_1):
     nc = tc.nc
     with ExitStack() as ctx:
+        moved = ctx.enter_context(tc.tile_pool(name="moved", bufs=1))
         keep = ctx.enter_context(tc.tile_pool(name="keep", bufs=1))
         grouping = ctx.enter_context(tc.tile_pool(name="grouping", bufs=6))
-        staging = ctx.enter_context(tc.tile_pool(name="staging", bufs=6))
         psum = ctx.enter_context(tc.psum_pool(name="psum", bufs=1))
         ctx.enter_context(tc.manual_schedule())
         vcopy, scopy = nc.vector.tensor_copy, nc.scalar.copy
@@ -39,31 +42,26 @@ def tile_rssmcell_pb_v_kernel(tc, h, embedding, wp1, bp1, wp2, bp2, wq1, bq1, wq
         def rows4(ap):
             return ap.rearrange("(p j) w -> p j w", j=PACK)
 
-        def load(name, view, dtype, queue=nc.sync):
-            raw = keep.tile([P] + list(view.shape[1:]), dtype, name=name, align_bytes=DMA_ALIGN)
+        def load(name, view, dtype, kib, queue=nc.sync):
+            raw = moved.tile([P] + list(view.shape[1:]), dtype, name=name, align_bytes=DMA_ALIGN, offset=kib * KIB)
             queue.dma_start(out=raw[:], in_=view)
             return raw
 
-        def operand(name):
-            codes = keep.tile([P, COLS], U32, name=name + "_codes", align_bytes=64)
-            scales = keep.tile([P, COLS], U8, name=name + "_scales", align_bytes=64)
+        def operand(name, width=COLS):
+            codes = keep.tile([P, width], U32, name=name + "_codes", align_bytes=64)
+            scales = keep.tile([P, width], U8, name=name + "_scales", align_bytes=64)
             return codes, scales
 
         def new_grouped():
             grouped = grouping.tile([P, COLS, PACK], BF16, name="grouped", align_bytes=64)
             return grouped
 
-        def new_bank(free):
+        free = list(range(8))
+
+        def new_bank():
             index = free.pop(0)
             bank = psum.tile([P, COLS], F32, name="bank%d" % index)
-            return bank, index, free
-
-        def release(held):
-            held[2].append(held[1])
-
-        def new_staged(rows, count):
-            staged = staging.tile([P, rows, count * COLS], F32, name="staged", align_bytes=DMA_ALIGN)
-            return staged
+            return bank, index
 
         def chunk(raw, n):
             return raw[:, :, COLS * n : COLS * (n + 1)]
@@ -76,12 +74,16 @@ def tile_rssmcell_pb_v_kernel(tc, h, embedding, wp1, bp1, wp2, bp2, wq1, bq1, wq
             interleave_into(copy, grouped[:], rows)
             return grouped
 
-        def quantize(target, grouped, fmt, cols=slice(0, COLS)):
+        made = set()
+
+        def quantize(target, grouped, fmt, name=None, cols=slice(None)):
             codes, scales = target
             nc.vector.quantize_mx(out=codes[:, cols].bitcast(fmt), scales=scales[:, cols], in_=grouped[:, cols, :].rearrange("p w t -> p (w t)"))
+            made.add(name)
+            fill()
 
-        def transpose_pair(words_of, pair, free):
-            held = new_bank(free)
+        def transpose_pair(words_of, pair):
+            held = new_bank()
             for jj in range(2):
                 for u in range(2):
                     at = P * (2 * jj + u)
@@ -97,7 +99,7 @@ def tile_rssmcell_pb_v_kernel(tc, h, embedding, wp1, bp1, wp2, bp2, wq1, bq1, wq
         def gather_pair(copy, grouped, pair, held):
             words = grouped[:].rearrange("p w t -> p (w t)").bitcast(F32)
             copy(out=words[:, COLS * pair : COLS * (pair + 1)].rearrange("p (j r u) -> p j r u", j=2, u=2), in_=held[0][:].rearrange("p (j u r) -> p j r u", j=2, u=2))
-            release(held)
+            free.append(held[1])
 
         def mx(held, stationary, m, moving, start, stop):
             cols = slice(P * m, P * (m + 1))
@@ -111,91 +113,126 @@ def tile_rssmcell_pb_v_kernel(tc, h, embedding, wp1, bp1, wp2, bp2, wq1, bq1, wq
                 stop=stop,
             )
 
-        def da_banks(g, free, js):
-            banks = []
-            for j in js:
-                bank = new_bank(free)
-                mx(bank, dz2_op, j, w2_op[g], True, True)
-                banks.append(bank)
-            return banks
+        def da_bank(g, j):
+            bank = new_bank()
+            mx(bank, dz2_op, j, w2_op[g], True, True)
+            return bank
 
-        def mask(g, j, banks, cols=slice(0, COLS)):
-            nc.vector.scalar_tensor_tensor(out=dz1[g][:, j, cols], in0=z_raw[j // 2][:, j % 2, COLS * g + cols.start : COLS * g + cols.stop], scalar=0.0, in1=banks[j][0][:, cols], op0=IS_GT, op1=MULT)
+        def mask(g, j, cols=slice(0, COLS)):
+            nc.vector.scalar_tensor_tensor(out=dz1[g][:, j, cols], in0=z_raw[j // 2][:, j % 2][:, COLS * g + cols.start : COLS * g + cols.stop], scalar=0.0, in1=da[g][j][0][:, cols], op0=IS_GT, op1=MULT)
             if cols.stop == COLS:
-                s_free.append(banks[j][1])
+                free.append(da[g][j][1])
+                made.add("dz1_%d_%d" % (g, j))
 
-        def empty(copy, staged, places, banks, last_first=True):
-            work = list(zip(places, banks))
-            for (r, at), bank in reversed(work) if last_first else work:
-                copy(out=staged[:, r, COLS * at : COLS * (at + 1)], in_=bank[0][:])
-                release(bank)
+        def tok_interleave(copy, k, g):
+            first, count = P * sum(GROUPS[:k]), GROUPS[k]
+            start, stop = max(first, COLS * g), min(first + P * count, COLS * (g + 1))
+            source = dz1[g][:, :, start - COLS * g : stop - COLS * g]
+            if count == 1:
+                interleave_into(copy, tok_grouped[k][:], source)
+            else:
+                target = tok_grouped[k][:].rearrange("p (r m) t -> p r m t", r=count)[:, :, (start - first) // count : (stop - first) // count, :]
+                copy(out=target.rearrange("p r (c i) t -> p c t i r", i=2), in_=source.rearrange("p t (c i r) -> p c t i r", r=count, i=2))
 
-        def out1_banks(pairs, free):
-            banks = []
-            for m, n in pairs:
-                bank = new_bank(free)
-                mx(bank, dz1_tok[m // 4], m % 4, c_op[n], True, True)
-                banks.append(bank)
-            return banks
+        waiting, filled, left = [], [], {}
 
-        def out0_banks(pairs, free):
-            banks = []
-            for j, n in pairs:
-                bank = new_bank(free)
-                for g in range(2):
-                    mx(bank, dz1_hid[g], j, w1_op[g][n], g == 0, g == 1)
-                banks.append(bank)
-            return banks
+        def fill():
+            while waiting and len(free) >= waiting[0][1] and waiting[0][0] <= made:
+                filled.extend(waiting.pop(0)[2]())
 
-        def store1(staged, m, rows, first, count):
-            view = out_1[P * m : P * (m + rows), COLS * first : COLS * (first + count)]
-            nc.sync.dma_start(out=view.rearrange("(r p) w -> p r w", p=P), in_=staged, max_dma_last_dim=2560)
+        def drain(copy, count=1, skip=0):
+            for step in range(count):
+                filled.pop(skip)(copy)
+                fill()
 
-        v_raw = load("v_raw", rows4(vq), F32, nc.scalar)
-        g1_raw = load("g1_raw", rows4(grad_1), BF16)
-        g0_raw = load("g0_raw", rows4(grad_0), BF16)
-        e_raw = load("e_raw", rows4(embedding), BF16)
-        w2_raw = load("w2_raw", rows4(wq2), BF16)
-        h_raw = load("h_raw", rows4(h), BF16)
-        z_raw = [load("z_raw%d" % pair, rows4(zq)[:, 2 * pair : 2 * pair + 2, :], F32) for pair in range(2)]
-        w_raw = []
-        for g in range(2):
-            raw = keep.tile([P, PACK, EMBED], BF16, name="w_raw%d" % g, align_bytes=DMA_ALIGN)
-            for js in (slice(0, 2), slice(2, 3), slice(3, 4)):
-                nc.sync.dma_start(out=raw[:, js, :], in_=rows4(wq1[COLS * g : COLS * (g + 1), DETER:])[:, js, :])
-            w_raw.append(raw)
+        def product_job(needs, name, view, places, passes):
+            def start():
+                held = [new_bank() for place in places]
+                for index, (stationary, moving) in enumerate(passes):
+                    for bank, (m, r, n) in zip(held, places):
+                        mx(bank, stationary, m, moving, index == 0, index == len(passes) - 1)
+                return [emptier(bank, r, n) for bank, (m, r, n) in zip(held, places)]
+
+            def emptier(bank, r, n):
+                def empty(copy):
+                    copy(out=staged_tile(name)[:, r, COLS * n : COLS * (n + 1)], in_=bank[0][:])
+                    free.append(bank[1])
+                    left[name] -= 1
+                    if left[name] == 0:
+                        nc.sync.dma_start(out=view, in_=staged_tile(name)[:])
+
+                return empty
+
+            left[name] = left.get(name, 0) + len(places)
+            waiting.append((needs, len(places), start))
+
+        def transpose_job(g, pair):
+            def start():
+                bank = transpose_pair(dz1_words(g), pair)
+                return [lambda copy: gather_pair(copy, hid_grouped[g], pair, bank)]
+
+            waiting.append(({"dz1_%d_%d" % (g, j) for j in (2 * pair, 2 * pair + 1)}, 1, start))
+
+        def out1_jobs(k, ns):
+            first, count = P * sum(GROUPS[:k]), GROUPS[k]
+            view = out_1[first : first + P * count, :].rearrange("(p r) w -> p r w", r=count)
+            for r in range(count):
+                for n in ns:
+                    product_job({"tok%d" % k, "c%d" % n}, "o1_%d" % k, view, [(r, r, n)], [(dz1_tok[k], c_op[n])])
+
+        def out0_job(pair, n):
+            passes = [(dz1_hid[g], w1_op[g][n]) for g in range(2)]
+            product_job({"hid0", "hid1", "w0%d" % n, "w1%d" % n}, "o0_%d" % pair, rows4(out_0)[:, 2 * pair : 2 * pair + 2, :], [(2 * pair + r, r, n) for r in range(2)], passes)
+
+        staged = {}
+
+        def staged_tile(name):
+            if name not in staged:
+                rows, width, kib = STAGED[name]
+                staged[name] = moved.tile([P, rows, width], F32, name=name, align_bytes=DMA_ALIGN, offset=kib * KIB)
+            return staged[name]
+
+        STAGED = {"o1_0": (1, CAT, 76), "o1_1": (1, CAT, 86), "o1_2": (2, CAT, 96), "o1_3": (2, CAT, 0), "o1_4": (2, CAT, 20), "o0_0": (2, EMBED, 76), "o0_1": (2, EMBED, 96)}
+
+        v_raw = load("v_raw", rows4(vq), F32, 44, nc.scalar)
+        g1_raw = load("g1_raw", rows4(grad_1), BF16, 48)
+        g0_raw = load("g0_raw", rows4(grad_0), BF16, 50)
+        w2_raw = load("w2_raw", rows4(wq2), BF16, 12)
+        e_raw = load("e_raw", rows4(embedding), BF16, 0)
+        z_raw = [load("z_raw%d" % pair, rows4(zq)[:, 2 * pair : 2 * pair + 2, :], F32, 28 + 8 * pair) for pair in range(2)]
+        h_raw = load("h_raw", rows4(h), BF16, 20)
+        w_raw = [load("w_raw%d" % g, rows4(wq1[COLS * g : COLS * (g + 1), DETER:]), BF16, 52 + 12 * g) for g in range(2)]
 
         ident = keep.tile([P, P], F32, name="ident")
         make_identity(nc, ident[:])
 
         w2_op = [operand("w2_0"), operand("w2_1")]
         dz2_op = operand("dz2")
-        dz1_tok = [operand("dz1_tok%d" % g) for g in range(2)]
+        dz1_tok = [operand("dz1_tok%d" % k, P * count) for k, count in enumerate(GROUPS)]
+        tok_grouped = [keep.tile([P, P * count, PACK], BF16, name="tok_grouped%d" % k, align_bytes=64) for k, count in enumerate(GROUPS)]
         dz1_hid = [operand("dz1_hid%d" % g) for g in range(2)]
         c_op = [operand("c%d" % n) for n in range(5)]
         w1_op = [[operand("w1_%d_%d" % (g, n)) for n in range(3)] for g in range(2)]
         dz1 = [keep.tile([P, PACK, COLS], BF16, name="dz1_%d" % g) for g in range(2)]
         dz2 = keep.tile([P, 2, PACK, STOC], BF16, name="dz2")
         sig = keep.tile([P, PACK, STOC], F32, name="sig")
-        s_free, v_free = [0, 1, 2, 3], [4, 5, 6, 7]
         halves = (slice(0, HALF), slice(HALF, COLS))
 
-        def w1_rows(n, g):
-            return interleave(vcopy, chunk(w_raw[g], n))
+        hid_grouped = [keep.tile([P, COLS, PACK], BF16, name="hid_grouped%d" % g, align_bytes=64) for g in range(2)]
 
-        def out1_part(copy, staged, m, ns, free, last_first=True):
-            banks = out1_banks([(m, n) for n in ns], free)
-            return lambda: empty(copy, staged, [(0, n) for n in ns], banks, last_first)
-
-        def out1_rows(m, copy=scopy, free=s_free):
-            staged = new_staged(1, 5)
-            out1_part(scopy, staged, m, (2, 3, 4), s_free)()
-            out1_part(copy, staged, m, (0, 1), free)()
-            store1(staged[:], m, 1, 0, 5)
-
-        def out0_pair(copy, pair, n, free, last_first=True):
-            banks = out0_banks([(2 * pair + r, n) for r in range(2)], free)
-            return lambda: empty(copy, out0_staged[pair], [(r, n) for r in range(2)], banks, last_first)
+        transpose_job(0, 0)
+        out1_jobs(0, (2, 3, 4, 0, 1))
+        out1_jobs(1, (2, 3, 4, 0, 1))
+        out1_jobs(2, (2, 3, 4, 0, 1))
+        out1_jobs(3, (0, 1, 2, 3, 4))
+        transpose_job(1, 0)
+        out1_jobs(4, (0,))
+        transpose_job(0, 1)
+        out1_jobs(4, (1,))
+        transpose_job(1, 1)
+        out1_jobs(4, (2, 3, 4))
+        for pair, n in ((0, 0), (1, 0), (0, 1), (0, 2), (1, 1), (1, 2)):
+            out0_job(pair, n)
 
         for pair in range(2):
             js = slice(2 * pair, 2 * pair + 2)
@@ -207,99 +244,105 @@ def tile_rssmcell_pb_v_kernel(tc, h, embedding, wp1, bp1, wp2, bp2, wq1, bq1, wq
                 op=MULT,
             )
         scopy(out=dz2[:, :, :, 0:P].bitcast(F32), in_=g0_raw[:].bitcast(F32).rearrange("p j (w u) -> p u j w", u=2))
-        banks = [transpose_pair(dz2_words, pair, s_free) for pair in range(2)]
+        banks = [transpose_pair(dz2_words, pair) for pair in range(2)]
         dz2_grouped = new_grouped()
         for pair in range(2):
             gather_pair(scopy, dz2_grouped, pair, banks[pair])
 
-        e_grouped = [interleave(vcopy, chunk(e_raw, 0)), new_grouped()]
-        quantize(dz2_op, dz2_grouped, E5M2)
+        w2_grouped = [interleave(vcopy, chunk(w2_raw, 0)), new_grouped()]
         for copy, cols in zip((vcopy, scopy), halves):
-            interleave_into(copy, e_grouped[1][:, cols, :], chunk(e_raw, 1)[:, :, cols])
-        quantize(c_op[2], e_grouped[0], E4M3)
-        e_grouped.append(interleave(scopy, chunk(e_raw, 2)))
-        w2_grouped = [interleave(copy, chunk(w2_raw, n)) for n, copy in enumerate((vcopy, scopy))]
-        quantize(c_op[3], e_grouped[1], E4M3)
+            interleave_into(copy, w2_grouped[1][:, cols, :], chunk(w2_raw, 1)[:, :, cols])
+        quantize(dz2_op, dz2_grouped, E5M2)
         quantize(w2_op[0], w2_grouped[0], E4M3)
-        quantize(c_op[4], e_grouped[2], E4M3)
-        h_grouped = [interleave(scopy, chunk(h_raw, n)) for n in range(2)]
-
-        da = [da_banks(0, v_free, range(PACK))]
+        da = [[da_bank(0, j) for j in range(PACK)]]
+        e_grouped = [interleave(vcopy, chunk(e_raw, 0)), None, interleave(scopy, chunk(e_raw, 2))]
+        e_grouped[1] = interleave(scopy, chunk(e_raw, 1))
         quantize(w2_op[1], w2_grouped[1], E4M3)
-        mask(0, 0, da[0])
-        mask(0, 1, da[0])
-        s_free.insert(0, s_free.pop())
-        da.append(da_banks(1, s_free, (0,)))
-        quantize(c_op[0], h_grouped[0], E4M3)
-        hid_grouped = [new_grouped()]
-        held = transpose_pair(dz1_words(0), 0, s_free)
-        da[1].extend(da_banks(1, s_free, (1,)))
-        first, second, rest = slice(0, P), slice(P, HALF), slice(P, COLS)
-        mask(0, 2, da[0], first)
-        mask(0, 3, da[0], first)
-        mask(0, 2, da[0], rest)
-        gather_pair(scopy, hid_grouped[0], 0, held)
-        s_free.insert(0, s_free.pop(-2))
-        da[1].extend(da_banks(1, s_free, (2,)))
-        tok_grouped = new_grouped()
-        interleave_into(vcopy, tok_grouped[:, first, :], dz1[0][:, :, first])
-        mask(0, 3, da[0], rest)
-        quantize(dz1_tok[0], tok_grouped, E5M2, first)
-        quantize(c_op[1], h_grouped[1], E4M3)
-        interleave_into(vcopy, tok_grouped[:, second, :], dz1[0][:, :, second])
-        third, fourth = slice(HALF, HALF + P), slice(HALF + P, COLS)
-        interleave_into(scopy, tok_grouped[:, third, :], dz1[0][:, :, third])
-        quantize(dz1_tok[0], tok_grouped, E5M2, second)
-        for m in range(2):
-            staged = new_staged(1, 5)
-            for n, copy in ((3, scopy), (4, scopy if m else vcopy), (2, vcopy if m else scopy), (0, scopy if m else vcopy), (1, scopy)):
-                out1_part(copy, staged, m, (n,), s_free)()
-            store1(staged[:], m, 1, 0, 5)
-            if m == 0:
-                interleave_into(vcopy, tok_grouped[:, fourth, :], dz1[0][:, :, fourth])
-                mask(1, 0, da[1])
-                quantize(dz1_tok[0], tok_grouped, E5M2, halves[1])
-        staged = new_staged(1, 5)
-        out1_part(scopy, staged, 2, (0, 1), s_free)()
-        da[1].extend(da_banks(1, s_free, (3,)))
-        for j in (1, 2):
-            mask(1, j, da[1])
-        out1_part(scopy, staged, 2, (2, 3, 4), s_free)()
-        store1(staged[:], 2, 1, 0, 5)
-        mask(1, 3, da[1])
-        v_free.extend([s_free.pop(0), s_free.pop()])
-        w_grouped = [new_grouped()]
-        interleave_into(vcopy, w_grouped[0][:, halves[0], :], chunk(w_raw[0], 0)[:, :, halves[0]])
-        tok_grouped = interleave(vcopy, dz1[1][:])
-        gather_pair(vcopy, hid_grouped[0], 1, transpose_pair(dz1_words(0), 1, v_free))
-        quantize(dz1_tok[1], tok_grouped, E5M2)
-        hid_grouped.append(new_grouped())
-        out1_rows(3)
-        gather_pair(vcopy, hid_grouped[1], 0, transpose_pair(dz1_words(1), 0, v_free))
-        interleave_into(vcopy, w_grouped[0][:, halves[1], :], chunk(w_raw[0], 0)[:, :, halves[1]])
-        quantize(dz1_hid[0], hid_grouped[0], E5M2)
-        quantize(w1_op[0][0], w_grouped[0], E4M3)
-        out1_rows(4, vcopy, v_free)
-        w_grouped.append(w1_rows(0, 1))
-        gather_pair(scopy, hid_grouped[1], 1, transpose_pair(dz1_words(1), 1, s_free))
-        out1_rows(5)
-        for step in range(1, 6):
-            if step < 5:
-                w_grouped.append(w1_rows((step + 1) // 2, (step + 1) % 2))
-            quantize(w1_op[step % 2][step // 2], w_grouped[step], E4M3)
-            if step == 1:
-                quantize(dz1_hid[1], hid_grouped[1], E5M2)
-        out1_rows(6)
-        early = out0_pair(vcopy, 1, 0, v_free)
-        out1_rows(7)
-
-        out0_staged = [new_staged(2, 3) for pair in range(2)]
-        out0_pair(scopy, 0, 0, s_free)()
-        out0_pair(scopy, 0, 1, s_free)()
-        late = out0_pair(scopy, 1, 1, s_free)
-        early()
-        out0_pair(vcopy, 0, 2, s_free, False)()
-        late()
-        out0_pair(vcopy, 1, 2, s_free, False)()
-        for pair in range(2):
-            nc.sync.dma_start(out=rows4(out_0)[:, 2 * pair : 2 * pair + 2, :], in_=out0_staged[pair][:])
+        da.append([da_bank(1, j) for j in range(2)])
+        quantize(c_op[2], e_grouped[0], E4M3, "c2")
+        mask(0, 0)
+        mask(0, 1)
+        quantize(c_op[4], e_grouped[2], E4M3, "c4")
+        drain(scopy)
+        mask(1, 0)
+        for k in range(2):
+            for j in (2, 3):
+                mask(0, j, slice(P * k, P * (k + 1)))
+            tok_interleave(scopy, k, 0)
+        quantize(c_op[3], e_grouped[1], E4M3, "c3")
+        da[1].append(da_bank(1, 2))
+        mask(1, 1)
+        da[1].append(da_bank(1, 3))
+        quantize(dz1_tok[0], tok_grouped[0], E5M2, "tok0")
+        h_grouped = [interleave(vcopy, chunk(h_raw, 0)), new_grouped()]
+        for copy, cols in zip((vcopy, scopy), (slice(0, P), slice(P, COLS))):
+            interleave_into(copy, h_grouped[1][:, cols, :], chunk(h_raw, 1)[:, :, cols])
+        quantize(c_op[0], h_grouped[0], E4M3, "c0")
+        drain(scopy)
+        quantize(c_op[1], h_grouped[1], E4M3, "c1")
+        quantize(dz1_tok[1], tok_grouped[1], E5M2, "tok1")
+        drain(scopy)
+        for j in (2, 3):
+            mask(0, j, halves[1])
+            fill()
+        drain(scopy, 2)
+        drain(vcopy)
+        tok_interleave(vcopy, 2, 0)
+        drain(scopy)
+        mask(1, 2, halves[0])
+        quantize(dz1_tok[2], tok_grouped[2], E5M2, "tok2")
+        drain(scopy)
+        mask(1, 3, halves[0])
+        drain(scopy, 2)
+        tok_interleave(vcopy, 3, 1)
+        drain(scopy)
+        drain(vcopy)
+        quantize(dz1_tok[3], tok_grouped[3], E5M2, "tok3")
+        drain(scopy)
+        for step in range(4):
+            drain(vcopy)
+            drain(scopy)
+        for j in (2, 3):
+            mask(1, j, halves[1])
+            fill()
+        drain(scopy)
+        w_grouped = [interleave(vcopy, chunk(w_raw[0], 0))]
+        drain(scopy, 2)
+        tok_interleave(vcopy, 4, 1)
+        drain(scopy)
+        drain(vcopy)
+        drain(scopy)
+        quantize(dz1_tok[4], tok_grouped[4], E5M2, "tok4")
+        drain(vcopy)
+        drain(scopy)
+        w_grouped.append(interleave(vcopy, chunk(w_raw[1], 0)))
+        drain(scopy, 2)
+        quantize(w1_op[0][0], w_grouped[0], E4M3, "w00")
+        drain(scopy)
+        quantize(w1_op[1][0], w_grouped[1], E4M3, "w10")
+        drain(vcopy)
+        drain(scopy)
+        w_grouped.append(interleave(vcopy, chunk(w_raw[0], 1)))
+        drain(scopy, 2)
+        w_grouped.append(interleave(vcopy, chunk(w_raw[1], 1)))
+        drain(scopy, 2)
+        quantize(dz1_hid[0], hid_grouped[0], E5M2, "hid0")
+        drain(scopy)
+        quantize(w1_op[0][1], w_grouped[2], E4M3, "w01")
+        drain(scopy)
+        quantize(dz1_hid[1], hid_grouped[1], E5M2, "hid1")
+        drain(scopy)
+        quantize(w1_op[1][1], w_grouped[3], E4M3, "w11")
+        drain(scopy)
+        w_grouped.append(interleave(vcopy, chunk(w_raw[0], 2)))
+        drain(scopy, 2)
+        w_grouped.append(interleave(vcopy, chunk(w_raw[1], 2)))
+        drain(scopy, 2)
+        drain(scopy, 2, 2)
+        quantize(w1_op[0][2], w_grouped[4], E4M3, "w02")
+        quantize(w1_op[1][2], w_grouped[5], E4M3, "w12")
+        drain(scopy, 2)
+        while filled:
+            drain(vcopy)
+            if filled:
+                drain(scopy)

@@ -180,9 +180,9 @@ def tile_rssmcell_pb_v_kernel(tc, h, embedding, wp1, bp1, wp2, bp2, wq1, bq1, wq
                 for n in ns:
                     product_job({"tok%d" % k, "c%d" % n}, "o1_%d" % k, view, [(r, r, n)], [(dz1_tok[k], c_op[n])])
 
-        def out0_job(pair, n):
+        def out0_job(js, n):
             passes = [(dz1_hid[g], w1_op[g][n]) for g in range(2)]
-            product_job({"hid0", "hid1", "w0%d" % n, "w1%d" % n}, "o0_%d" % pair, rows4(out_0)[:, 2 * pair : 2 * pair + 2, :], [(2 * pair + r, r, n) for r in range(2)], passes)
+            product_job({"hid0", "hid1", "w0%d" % n, "w1%d" % n}, "o0", rows4(out_0), [(j, j, n) for j in js], passes)
 
         staged = {}
 
@@ -192,7 +192,7 @@ def tile_rssmcell_pb_v_kernel(tc, h, embedding, wp1, bp1, wp2, bp2, wq1, bq1, wq
                 staged[name] = moved.tile([P, rows, width], F32, name=name, align_bytes=DMA_ALIGN, offset=kib * KIB)
             return staged[name]
 
-        STAGED = {"o1_0": (1, CAT, 76), "o1_1": (1, CAT, 86), "o1_2": (2, CAT, 96), "o1_3": (2, CAT, 0), "o1_4": (2, CAT, 20), "o0_0": (2, EMBED, 76), "o0_1": (2, EMBED, 96)}
+        STAGED = {"o1_0": (1, CAT, 76), "o1_1": (1, CAT, 86), "o1_2": (2, CAT, 96), "o1_3": (2, CAT, 0), "o1_4": (2, CAT, 20), "o0": (4, EMBED, 76)}
 
         v_raw = load("v_raw", rows4(vq), F32, 44, nc.scalar)
         g1_raw = load("g1_raw", rows4(grad_1), BF16, 48)
@@ -221,18 +221,19 @@ def tile_rssmcell_pb_v_kernel(tc, h, embedding, wp1, bp1, wp2, bp2, wq1, bq1, wq
         hid_grouped = [keep.tile([P, COLS, PACK], BF16, name="hid_grouped%d" % g, align_bytes=64) for g in range(2)]
 
         transpose_job(0, 0)
+        transpose_job(1, 0)
         out1_jobs(0, (2, 3, 4, 0, 1))
         out1_jobs(1, (2, 3, 4, 0, 1))
         out1_jobs(2, (2, 3, 4, 0, 1))
         out1_jobs(3, (0, 1, 2, 3, 4))
-        transpose_job(1, 0)
-        out1_jobs(4, (0,))
         transpose_job(0, 1)
-        out1_jobs(4, (1,))
+        out1_jobs(4, (0,))
         transpose_job(1, 1)
-        out1_jobs(4, (2, 3, 4))
-        for pair, n in ((0, 0), (1, 0), (0, 1), (0, 2), (1, 1), (1, 2)):
-            out0_job(pair, n)
+        out1_jobs(4, (1, 2, 3, 4))
+        for n in range(2):
+            out0_job((0, 1), n)
+            out0_job((2, 3), n)
+        out0_job(range(PACK), 2)
 
         for pair in range(2):
             js = slice(2 * pair, 2 * pair + 2)
@@ -249,34 +250,38 @@ def tile_rssmcell_pb_v_kernel(tc, h, embedding, wp1, bp1, wp2, bp2, wq1, bq1, wq
         for pair in range(2):
             gather_pair(scopy, dz2_grouped, pair, banks[pair])
 
-        w2_grouped = [interleave(vcopy, chunk(w2_raw, 0)), new_grouped()]
-        for copy, cols in zip((vcopy, scopy), halves):
-            interleave_into(copy, w2_grouped[1][:, cols, :], chunk(w2_raw, 1)[:, :, cols])
+        quarter, rest = slice(0, P), slice(P, COLS)
+
+        def interleave_shared(rows):
+            grouped = new_grouped()
+            for copy, cols in ((vcopy, quarter), (scopy, rest)):
+                interleave_into(copy, grouped[:, cols, :], rows[:, :, cols])
+            return grouped
+
+        w2_grouped = [interleave(vcopy, chunk(w2_raw, 0)), interleave_shared(chunk(w2_raw, 1))]
         quantize(dz2_op, dz2_grouped, E5M2)
         quantize(w2_op[0], w2_grouped[0], E4M3)
         da = [[da_bank(0, j) for j in range(PACK)]]
-        e_grouped = [interleave(vcopy, chunk(e_raw, 0)), None, interleave(scopy, chunk(e_raw, 2))]
-        e_grouped[1] = interleave(scopy, chunk(e_raw, 1))
         quantize(w2_op[1], w2_grouped[1], E4M3)
         da.append([da_bank(1, j) for j in range(2)])
+        e_grouped = [interleave(vcopy, chunk(e_raw, 0)), None, interleave(scopy, chunk(e_raw, 2))]
+        e_grouped[1] = interleave_shared(chunk(e_raw, 1))
         quantize(c_op[2], e_grouped[0], E4M3, "c2")
-        mask(0, 0)
-        mask(0, 1)
-        quantize(c_op[4], e_grouped[2], E4M3, "c4")
+        for g in range(2):
+            mask(g, 0)
+            mask(g, 1)
+            fill()
         drain(scopy)
-        mask(1, 0)
         for k in range(2):
             for j in (2, 3):
                 mask(0, j, slice(P * k, P * (k + 1)))
             tok_interleave(scopy, k, 0)
+        quantize(c_op[4], e_grouped[2], E4M3, "c4")
+        da[1].extend(da_bank(1, j) for j in (2, 3))
         quantize(c_op[3], e_grouped[1], E4M3, "c3")
-        da[1].append(da_bank(1, 2))
-        mask(1, 1)
-        da[1].append(da_bank(1, 3))
+        drain(scopy)
         quantize(dz1_tok[0], tok_grouped[0], E5M2, "tok0")
-        h_grouped = [interleave(vcopy, chunk(h_raw, 0)), new_grouped()]
-        for copy, cols in zip((vcopy, scopy), (slice(0, P), slice(P, COLS))):
-            interleave_into(copy, h_grouped[1][:, cols, :], chunk(h_raw, 1)[:, :, cols])
+        h_grouped = [interleave(vcopy, chunk(h_raw, 0)), interleave_shared(chunk(h_raw, 1))]
         quantize(c_op[0], h_grouped[0], E4M3, "c0")
         drain(scopy)
         quantize(c_op[1], h_grouped[1], E4M3, "c1")
@@ -310,16 +315,13 @@ def tile_rssmcell_pb_v_kernel(tc, h, embedding, wp1, bp1, wp2, bp2, wq1, bq1, wq
         drain(scopy, 2)
         tok_interleave(vcopy, 4, 1)
         drain(scopy)
-        drain(vcopy)
-        drain(scopy)
-        quantize(dz1_tok[4], tok_grouped[4], E5M2, "tok4")
-        drain(vcopy)
-        drain(scopy)
         w_grouped.append(interleave(vcopy, chunk(w_raw[1], 0)))
         drain(scopy, 2)
+        quantize(dz1_tok[4], tok_grouped[4], E5M2, "tok4")
         quantize(w1_op[0][0], w_grouped[0], E4M3, "w00")
-        drain(scopy)
+        drain(scopy, 2)
         quantize(w1_op[1][0], w_grouped[1], E4M3, "w10")
+        drain(scopy)
         drain(vcopy)
         drain(scopy)
         w_grouped.append(interleave(vcopy, chunk(w_raw[0], 1)))
@@ -328,20 +330,25 @@ def tile_rssmcell_pb_v_kernel(tc, h, embedding, wp1, bp1, wp2, bp2, wq1, bq1, wq
         drain(scopy, 2)
         quantize(dz1_hid[0], hid_grouped[0], E5M2, "hid0")
         drain(scopy)
-        quantize(w1_op[0][1], w_grouped[2], E4M3, "w01")
-        drain(scopy)
         quantize(dz1_hid[1], hid_grouped[1], E5M2, "hid1")
+        drain(vcopy)
+        drain(scopy)
+        quantize(w1_op[0][1], w_grouped[2], E4M3, "w01")
         drain(scopy)
         quantize(w1_op[1][1], w_grouped[3], E4M3, "w11")
         drain(scopy)
         w_grouped.append(interleave(vcopy, chunk(w_raw[0], 2)))
+        w_grouped.append(new_grouped())
         drain(scopy, 2)
-        w_grouped.append(interleave(vcopy, chunk(w_raw[1], 2)))
-        drain(scopy, 2)
-        drain(scopy, 2, 2)
+        interleave_into(vcopy, w_grouped[5][:, halves[0], :], chunk(w_raw[1], 2)[:, :, halves[0]])
+        drain(scopy)
         quantize(w1_op[0][2], w_grouped[4], E4M3, "w02")
-        quantize(w1_op[1][2], w_grouped[5], E4M3, "w12")
-        drain(scopy, 2)
+        drain(scopy)
+        interleave_into(vcopy, w_grouped[5][:, halves[1], :], chunk(w_raw[1], 2)[:, :, halves[1]])
+        drain(scopy)
+        quantize(w1_op[1][2], w_grouped[5], E4M3, None, halves[0])
+        quantize(w1_op[1][2], w_grouped[5], E4M3, "w12", halves[1])
+        drain(scopy, 4)
         while filled:
             drain(vcopy)
             if filled:

@@ -25,6 +25,7 @@ PACK = 4
 COLS = 512
 HALF = COLS // 2
 DMA_ALIGN = 256
+POOL_ALIGN = 4096
 KIB = 1024
 GROUPS = (1, 1, 2, 2, 2)
 
@@ -43,7 +44,7 @@ def tile_rssmcell_pb_v_kernel(tc, h, embedding, wp1, bp1, wp2, bp2, wq1, bq1, wq
             return ap.rearrange("(p j) w -> p j w", j=PACK)
 
         def load(name, view, dtype, kib, queue=nc.sync):
-            raw = moved.tile([P] + list(view.shape[1:]), dtype, name=name, align_bytes=DMA_ALIGN, offset=kib * KIB)
+            raw = moved.tile([P] + list(view.shape[1:]), dtype, name=name, align_bytes=DMA_ALIGN if kib else POOL_ALIGN, offset=kib * KIB)
             queue.dma_start(out=raw[:], in_=view)
             return raw
 

@@ -1,7 +1,6 @@
 from contextlib import ExitStack
 
 import concourse.mybir as mybir
-from concourse.masks import make_identity
 
 B, EMBED, DETER, STOC, HID = 512, 1536, 1024, 256, 1024
 DIST = 2 * STOC
@@ -18,6 +17,8 @@ E4M3 = mybir.dt.float8_e4m3fn_x4
 E5M2 = mybir.dt.float8_e5m2_x4
 MULT = mybir.AluOpType.mult
 IS_GT = mybir.AluOpType.is_gt
+IS_EQUAL = mybir.AluOpType.is_equal
+ADD = mybir.AluOpType.add
 SIGMOID = mybir.ActivationFunctionType.Sigmoid
 
 P = 128
@@ -205,7 +206,14 @@ def tile_rssmcell_pb_v_kernel(tc, h, embedding, wp1, bp1, wp2, bp2, wq1, bq1, wq
         w_raw = [load("w_raw%d" % g, rows4(wq1[COLS * g : COLS * (g + 1), DETER:]), BF16, 52 + 12 * g) for g in range(2)]
 
         ident = keep.tile([P, P], F32, name="ident")
-        make_identity(nc, ident[:])
+        ones = keep.tile([P, P], F32, name="ones")
+        column = keep.tile([P, P], F32, name="column", align_bytes=64)
+        turned = keep.tile([P, P], F32, name="turned", align_bytes=64)
+        nc.vector.memset(ones[:], 1.0)
+        nc.vector.tensor_tensor_scan(out=column[:], data0=ones[:], data1=ones[:], initial=0.0, op0=MULT, op1=ADD)
+        nc.vector.transpose(out=turned[:], in_=column[:])
+        for q in range(0, P, 32):
+            nc.vector.tensor_scalar(out=ident[q : q + 32, :], in0=column[q : q + 32, :], scalar1=turned[q : q + 32, q : q + 1], scalar2=None, op0=IS_EQUAL)
 
         w2_op = [operand("w2_0"), operand("w2_1")]
         dz2_op = operand("dz2")

from contextlib import ExitStack

import concourse.mybir as mybir

B, EMBED, DETER, STOC, HID = 512, 1536, 1024, 256, 1024
DIST = 2 * STOC
CAT = DETER + EMBED

FLOPS = 2 * (B * DIST * HID + B * HID * EMBED + HID * B * CAT)
BYTES = 2 * (2 * B * STOC + DIST * HID + HID * EMBED + B * CAT) + 4 * (B * STOC + B * HID) + 4 * (B * EMBED + HID * CAT)

F32 = mybir.dt.float32
BF16 = mybir.dt.bfloat16
U32 = mybir.dt.uint32
U8 = mybir.dt.uint8
E4M3 = mybir.dt.float8_e4m3fn_x4
E5M2 = mybir.dt.float8_e5m2_x4
MULT = mybir.AluOpType.mult
IS_GT = mybir.AluOpType.is_gt
IS_EQUAL = mybir.AluOpType.is_equal
ADD = mybir.AluOpType.add
SIGMOID = mybir.ActivationFunctionType.Sigmoid

P = 128
PACK = 4
COLS = 512
HALF = COLS // 2
DMA_ALIGN = 256
POOL_ALIGN = 4096
KIB = 1024
GROUPS = (1, 1, 2, 2, 2)


def tile_rssmcell_pb_v_kernel(tc, h, embedding, wp1, bp1, wp2, bp2, wq1, bq1, wq2, bq2, zq, vq, grad_0, grad_1, grad_2, grad_3, out_0, out_1):
    nc = tc.nc
    with ExitStack() as ctx:
        moved = ctx.enter_context(tc.tile_pool(name="moved", bufs=1))
        keep = ctx.enter_context(tc.tile_pool(name="keep", bufs=1))
        grouping = ctx.enter_context(tc.tile_pool(name="grouping", bufs=6))
        psum = ctx.enter_context(tc.psum_pool(name="psum", bufs=1))
        ctx.enter_context(tc.manual_schedule())
        vcopy, scopy = nc.vector.tensor_copy, nc.scalar.copy

        def rows4(ap):
            return ap.rearrange("(p j) w -> p j w", j=PACK)

        def load(name, view, dtype, kib, queue=nc.sync):
            raw = moved.tile([P] + list(view.shape[1:]), dtype, name=name, align_bytes=DMA_ALIGN if kib else POOL_ALIGN, offset=kib * KIB)
            queue.dma_start(out=raw[:], in_=view)
            return raw

        def operand(name, width=COLS):
            codes = keep.tile([P, width], U32, name=name + "_codes", align_bytes=64)
            scales = keep.tile([P, width], U8, name=name + "_scales", align_bytes=64)
            return codes, scales

        def new_grouped():
            grouped = grouping.tile([P, COLS, PACK], BF16, name="grouped", align_bytes=64)
            return grouped

        free = list(range(8))

        def new_bank():
            index = free.pop(0)
            bank = psum.tile([P, COLS], F32, name="bank%d" % index)
            return bank, index

        def chunk(raw, n):
            return raw[:, :, COLS * n : COLS * (n + 1)]

        def interleave_into(copy, grouped, rows):
            copy(out=grouped.rearrange("p (c i) t -> p c t i", i=4), in_=rows.rearrange("p t (c i) -> p c t i", i=4))

        def interleave(copy, rows):
            grouped = new_grouped()
            interleave_into(copy, grouped[:], rows)
            return grouped

        made = set()

        def quantize(target, grouped, fmt, name=None, cols=slice(None)):
            codes, scales = target
            nc.vector.quantize_mx(out=codes[:, cols].bitcast(fmt), scales=scales[:, cols], in_=grouped[:, cols, :].rearrange("p w t -> p (w t)"))
            made.add(name)
            fill()

        def transpose_pair(words_of, pair):
            held = new_bank()
            for jj in range(2):
                for u in range(2):
                    at = P * (2 * jj + u)
                    nc.tensor.transpose(held[0][:, at : at + P], words_of(2 * pair + jj, u), ident[:])
            return held

        def dz2_words(j, u):
            return dz2[:, u, j, :].bitcast(F32)

        def dz1_words(g):
            return lambda j, u: dz1[g][:, j, :].bitcast(F32)[:, u::2]

        def gather_pair(copy, grouped, pair, held):
            words = grouped[:].rearrange("p w t -> p (w t)").bitcast(F32)
            copy(out=words[:, COLS * pair : COLS * (pair + 1)].rearrange("p (j r u) -> p j r u", j=2, u=2), in_=held[0][:].rearrange("p (j u r) -> p j r u", j=2, u=2))
            free.append(held[1])

        def mx(held, stationary, m, moving, start, stop):
            cols = slice(P * m, P * (m + 1))
            nc.tensor.matmul_mx(
                out=held[0][:],
                lhsT=stationary[0][:, cols].bitcast(E5M2),
                lhsT_scale=stationary[1][:, cols],
                rhs=moving[0][:].bitcast(E4M3),
                rhs_scale=moving[1][:],
                start=start,
                stop=stop,
            )

        def da_bank(g, j):
            bank = new_bank()
            mx(bank, dz2_op, j, w2_op[g], True, True)
            return bank

        def mask(g, j, cols=slice(0, COLS)):
            nc.vector.scalar_tensor_tensor(out=dz1[g][:, j, cols], in0=z_raw[j // 2][:, j % 2][:, COLS * g + cols.start : COLS * g + cols.stop], scalar=0.0, in1=da[g][j][0][:, cols], op0=IS_GT, op1=MULT)
            if cols.stop == COLS:
                free.append(da[g][j][1])
                made.add("dz1_%d_%d" % (g, j))

        def tok_interleave(copy, k, g):
            first, count = P * sum(GROUPS[:k]), GROUPS[k]
            start, stop = max(first, COLS * g), min(first + P * count, COLS * (g + 1))
            source = dz1[g][:, :, start - COLS * g : stop - COLS * g]
            if count == 1:
                interleave_into(copy, tok_grouped[k][:], source)
            else:
                target = tok_grouped[k][:].rearrange("p (r m) t -> p r m t", r=count)[:, :, (start - first) // count : (stop - first) // count, :]
                copy(out=target.rearrange("p r (c i) t -> p c t i r", i=2), in_=source.rearrange("p t (c i r) -> p c t i r", r=count, i=2))

        waiting, filled, left = [], [], {}

        def fill():
            while waiting and len(free) >= waiting[0][1] and waiting[0][0] <= made:
                filled.extend(waiting.pop(0)[2]())

        def drain(copy, count=1, skip=0):
            for step in range(count):
                filled.pop(skip)(copy)
                fill()

        def product_job(needs, name, view, places, passes):
            def start():
                held = [new_bank() for place in places]
                for index, (stationary, moving) in enumerate(passes):
                    for bank, (m, r, n) in zip(held, places):
                        mx(bank, stationary, m, moving, index == 0, index == len(passes) - 1)
                return [emptier(bank, r, n) for bank, (m, r, n) in zip(held, places)]

            def emptier(bank, r, n):
                def empty(copy):
                    copy(out=staged_tile(name)[:, r, COLS * n : COLS * (n + 1)], in_=bank[0][:])
                    free.append(bank[1])
                    left[name] -= 1
                    if left[name] == 0:
                        nc.sync.dma_start(out=view, in_=staged_tile(name)[:])

                return empty

            left[name] = left.get(name, 0) + len(places)
            waiting.append((needs, len(places), start))

        def transpose_job(g, pair):
            def start():
                bank = transpose_pair(dz1_words(g), pair)
                return [lambda copy: gather_pair(copy, hid_grouped[g], pair, bank)]

            waiting.append(({"dz1_%d_%d" % (g, j) for j in (2 * pair, 2 * pair + 1)}, 1, start))

        def out1_jobs(k, ns):
            first, count = P * sum(GROUPS[:k]), GROUPS[k]
            view = out_1[first : first + P * count, :].rearrange("(p r) w -> p r w", r=count)
            for r in range(count):
                for n in ns:
                    product_job({"tok%d" % k, "c%d" % n}, "o1_%d" % k, view, [(r, r, n)], [(dz1_tok[k], c_op[n])])

        def out0_job(js, n):
            passes = [(dz1_hid[g], w1_op[g][n]) for g in range(2)]
            product_job({"hid0", "hid1", "w0%d" % n, "w1%d" % n}, "o0", rows4(out_0), [(j, j, n) for j in js], passes)

        staged = {}

        def staged_tile(name):
            if name not in staged:
                rows, width, kib = STAGED[name]
                staged[name] = moved.tile([P, rows, width], F32, name=name, align_bytes=DMA_ALIGN, offset=kib * KIB)
            return staged[name]

        STAGED = {"o1_0": (1, CAT, 76), "o1_1": (1, CAT, 86), "o1_2": (2, CAT, 96), "o1_3": (2, CAT, 0), "o1_4": (2, CAT, 20), "o0": (4, EMBED, 76)}

        v_raw = load("v_raw", rows4(vq), F32, 44, nc.scalar)
        g1_raw = load("g1_raw", rows4(grad_1), BF16, 48)
        g0_raw = load("g0_raw", rows4(grad_0), BF16, 50)
        w2_raw = load("w2_raw", rows4(wq2), BF16, 12)
        e_raw = load("e_raw", rows4(embedding), BF16, 0)
        z_raw = [load("z_raw%d" % pair, rows4(zq)[:, 2 * pair : 2 * pair + 2, :], F32, 28 + 8 * pair) for pair in range(2)]
        h_raw = load("h_raw", rows4(h), BF16, 20)
        w_raw = [load("w_raw%d" % g, rows4(wq1[COLS * g : COLS * (g + 1), DETER:]), BF16, 52 + 12 * g) for g in range(2)]

        ident = keep.tile([P, P], F32, name="ident")
        ones = keep.tile([P, P], F32, name="ones")
        column = keep.tile([P, P], F32, name="column", align_bytes=64)
        turned = keep.tile([P, P], F32, name="turned", align_bytes=64)
        nc.vector.memset(ones[:], 1.0)
        nc.vector.tensor_tensor_scan(out=column[:], data0=ones[:], data1=ones[:], initial=0.0, op0=MULT, op1=ADD)
        nc.vector.transpose(out=turned[:], in_=column[:])
        for q in range(0, P, 32):
            nc.vector.tensor_scalar(out=ident[q : q + 32, :], in0=column[q : q + 32, :], scalar1=turned[q : q + 32, q : q + 1], scalar2=None, op0=IS_EQUAL)

        w2_op = [operand("w2_0"), operand("w2_1")]
        dz2_op = operand("dz2")
        dz1_tok = [operand("dz1_tok%d" % k, P * count) for k, count in enumerate(GROUPS)]
        tok_grouped = [keep.tile([P, P * count, PACK], BF16, name="tok_grouped%d" % k, align_bytes=64) for k, count in enumerate(GROUPS)]
        dz1_hid = [operand("dz1_hid%d" % g) for g in range(2)]
        c_op = [operand("c%d" % n) for n in range(5)]
        w1_op = [[operand("w1_%d_%d" % (g, n)) for n in range(3)] for g in range(2)]
        dz1 = [keep.tile([P, PACK, COLS], BF16, name="dz1_%d" % g) for g in range(2)]
        dz2 = keep.tile([P, 2, PACK, STOC], BF16, name="dz2")
        sig = keep.tile([P, PACK, STOC], F32, name="sig")
        halves = (slice(0, HALF), slice(HALF, COLS))

        hid_grouped = [keep.tile([P, COLS, PACK], BF16, name="hid_grouped%d" % g, align_bytes=64) for g in range(2)]

        transpose_job(0, 0)
        transpose_job(1, 0)
        out1_jobs(0, (2, 3, 4, 0, 1))
        out1_jobs(1, (2, 3, 4, 0, 1))
        out1_jobs(2, (2, 3, 4, 0, 1))
        out1_jobs(3, (0, 1, 2, 3, 4))
        transpose_job(0, 1)
        out1_jobs(4, (0,))
        transpose_job(1, 1)
        out1_jobs(4, (1, 2, 3, 4))
        for n in range(2):
            out0_job((0, 1), n)
            out0_job((2, 3), n)
        out0_job(range(PACK), 2)

        for pair in range(2):
            js = slice(2 * pair, 2 * pair + 2)
            nc.scalar.activation(out=sig[:, js, :], in_=v_raw[:, js, :], func=SIGMOID)
            nc.vector.tensor_tensor(
                out=dz2[:, :, js, P:].rearrange("p u j (w e) -> p u j w e", e=2),
                in0=g1_raw[:, js, :].rearrange("p j (w u e) -> p u j w e", u=2, e=2),
                in1=sig[:, js, :].rearrange("p j (w u e) -> p u j w e", u=2, e=2),
                op=MULT,
            )
        scopy(out=dz2[:, :, :, 0:P].bitcast(F32), in_=g0_raw[:].bitcast(F32).rearrange("p j (w u) -> p u j w", u=2))
        banks = [transpose_pair(dz2_words, pair) for pair in range(2)]
        dz2_grouped = new_grouped()
        for pair in range(2):
            gather_pair(scopy, dz2_grouped, pair, banks[pair])

        quarter, rest = slice(0, P), slice(P, COLS)

        def interleave_shared(rows):
            grouped = new_grouped()
            for copy, cols in ((vcopy, quarter), (scopy, rest)):
                interleave_into(copy, grouped[:, cols, :], rows[:, :, cols])
            return grouped

        w2_grouped = [interleave(vcopy, chunk(w2_raw, 0)), interleave_shared(chunk(w2_raw, 1))]
        quantize(dz2_op, dz2_grouped, E5M2)
        quantize(w2_op[0], w2_grouped[0], E4M3)
        da = [[da_bank(0, j) for j in range(PACK)]]
        quantize(w2_op[1], w2_grouped[1], E4M3)
        da.append([da_bank(1, j) for j in range(2)])
        e_grouped = [interleave(vcopy, chunk(e_raw, 0)), None, interleave(scopy, chunk(e_raw, 2))]
        e_grouped[1] = interleave_shared(chunk(e_raw, 1))
        quantize(c_op[2], e_grouped[0], E4M3, "c2")
        for g in range(2):
            mask(g, 0)
            mask(g, 1)
            fill()
        drain(scopy)
        for k in range(2):
            for j in (2, 3):
                mask(0, j, slice(P * k, P * (k + 1)))
            tok_interleave(scopy, k, 0)
        quantize(c_op[4], e_grouped[2], E4M3, "c4")
        da[1].extend(da_bank(1, j) for j in (2, 3))
        quantize(c_op[3], e_grouped[1], E4M3, "c3")
        drain(scopy)
        quantize(dz1_tok[0], tok_grouped[0], E5M2, "tok0")
        h_grouped = [interleave(vcopy, chunk(h_raw, 0)), interleave_shared(chunk(h_raw, 1))]
        quantize(c_op[0], h_grouped[0], E4M3, "c0")
        drain(scopy)
        quantize(c_op[1], h_grouped[1], E4M3, "c1")
        quantize(dz1_tok[1], tok_grouped[1], E5M2, "tok1")
        drain(scopy)
        for j in (2, 3):
            mask(0, j, halves[1])
            fill()
        drain(scopy, 2)
        drain(vcopy)
        tok_interleave(vcopy, 2, 0)
        drain(scopy)
        mask(1, 2, halves[0])
        quantize(dz1_tok[2], tok_grouped[2], E5M2, "tok2")
        drain(scopy)
        mask(1, 3, halves[0])
        drain(scopy, 2)
        tok_interleave(vcopy, 3, 1)
        drain(scopy)
        drain(vcopy)
        quantize(dz1_tok[3], tok_grouped[3], E5M2, "tok3")
        drain(scopy)
        for step in range(4):
            drain(vcopy)
            drain(scopy)
        for j in (2, 3):
            mask(1, j, halves[1])
            fill()
        drain(scopy)
        w_grouped = [interleave(vcopy, chunk(w_raw[0], 0))]
        drain(scopy, 2)
        tok_interleave(vcopy, 4, 1)
        drain(scopy)
        w_grouped.append(interleave(vcopy, chunk(w_raw[1], 0)))
        drain(scopy, 2)
        quantize(dz1_tok[4], tok_grouped[4], E5M2, "tok4")
        quantize(w1_op[0][0], w_grouped[0], E4M3, "w00")
        drain(scopy, 2)
        quantize(w1_op[1][0], w_grouped[1], E4M3, "w10")
        drain(scopy)
        drain(vcopy)
        drain(scopy)
        w_grouped.append(interleave(vcopy, chunk(w_raw[0], 1)))
        drain(scopy, 2)
        w_grouped.append(interleave(vcopy, chunk(w_raw[1], 1)))
        drain(scopy, 2)
        quantize(dz1_hid[0], hid_grouped[0], E5M2, "hid0")
        drain(scopy)
        quantize(dz1_hid[1], hid_grouped[1], E5M2, "hid1")
        drain(vcopy)
        drain(scopy)
        quantize(w1_op[0][1], w_grouped[2], E4M3, "w01")
        drain(scopy)
        quantize(w1_op[1][1], w_grouped[3], E4M3, "w11")
        drain(scopy)
        w_grouped.append(interleave(vcopy, chunk(w_raw[0], 2)))
        w_grouped.append(new_grouped())
        drain(scopy, 2)
        interleave_into(vcopy, w_grouped[5][:, halves[0], :], chunk(w_raw[1], 2)[:, :, halves[0]])
        drain(scopy)
        quantize(w1_op[0][2], w_grouped[4], E4M3, "w02")
        drain(scopy)
        interleave_into(vcopy, w_grouped[5][:, halves[1], :], chunk(w_raw[1], 2)[:, :, halves[1]])
        drain(scopy)
        quantize(w1_op[1][2], w_grouped[5], E4M3, None, halves[0])
        quantize(w1_op[1][2], w_grouped[5], E4M3, "w12", halves[1])
        drain(scopy, 4)
        while filled:
            drain(vcopy)
            if filled:
                drain(scopy)
